import numpy as np
import ml_dtypes


def mxq(x, axis, fmt="e4m3"):
    dtype, down = {"e4m3": (ml_dtypes.float8_e4m3fn, 7), "e5m2": (ml_dtypes.float8_e5m2, 14)}[fmt]
    v = np.moveaxis(np.asarray(x, np.float32).astype(ml_dtypes.bfloat16).astype(np.float64), axis, -1)
    blocks = v.reshape(v.shape[:-1] + (-1, 32))
    amax = np.abs(blocks).max(-1, keepdims=True)
    byte = np.maximum(np.where(amax > 0, np.frexp(amax)[1] - 1 + 127, 0) - down, 1)
    scale = np.exp2(byte - 127.0)
    codes = (blocks / scale).astype(np.float32).astype(dtype).astype(np.float64)
    return np.moveaxis((codes * scale).reshape(v.shape), -1, axis)


WIDE = False


def mx_kscale(k):
    if not WIDE:
        return np.ones(k)
    levels = np.array([10, -10, 5, -5, 0])
    a = np.random.permutation(np.resize(levels, k // 512 * 4)).reshape(k // 512, 4)
    idx = np.arange(k)
    return np.exp2(a[idx // 512, idx % 128 // 32])


BF16 = ml_dtypes.bfloat16


def bf(x):
    return np.asarray(x, np.float32).astype(BF16)


def f64(x):
    return np.asarray(x).astype(np.float64)


E2M1 = np.array([0.0, 0.5, 1.0, 1.5, 2.0, 3.0, 4.0, 6.0, -0.0, -0.5, -1.0, -1.5, -2.0, -3.0, -4.0, -6.0])


def pack_weight(w, fmt):
    k, n = w.shape
    w = f64(bf(w)).reshape(k // 32, 32, n)
    amax = np.abs(w).max(1)
    if fmt == "e4m3":
        byte = np.frexp(amax)[1] - 1 + 127 - 7
    else:
        mant, ex = np.frexp(amax / 6.0)
        byte = np.where(mant > 0.5, ex, ex - 1) + 127
    byte = np.clip(np.where(amax > 0, byte, 1), 1, 254)
    scaled = (w * np.exp2(127.0 - byte)[:, None, :]).reshape(k, n).astype(np.float32)
    by_word = np.ascontiguousarray(scaled.reshape(k // 512, 128, 4, n).transpose(0, 1, 3, 2))
    if fmt == "e4m3":
        words = by_word.astype(ml_dtypes.float8_e4m3fn).view(np.uint8)
    else:
        c = by_word.astype(ml_dtypes.float4_e2m1fn).view(np.uint8) & 0xF
        words = c[..., 0::2] | (c[..., 1::2] << 4)
    return np.ascontiguousarray(words), np.ascontiguousarray(byte.astype(np.uint8).reshape(k // 512, 16, n))


def unpack_weight(words, scales, fmt):
    g, p, n, _ = words.shape
    if fmt == "e4m3":
        vals = np.ascontiguousarray(words).view(ml_dtypes.float8_e4m3fn).astype(np.float64)
    else:
        nib = np.empty((g, p, n, 4), np.uint8)
        nib[..., 0::2] = words & 0xF
        nib[..., 1::2] = words >> 4
        vals = E2M1[nib]
    vals = vals * np.repeat(np.exp2(scales.astype(np.float64) - 127.0), 8, axis=1)[..., None]
    return vals.transpose(0, 1, 3, 2).reshape(g * 512, n)


B, P, D, NL, T, E, G = 2, 192, 1024, 16, 2, 1, 2
WG = NL * NL * T * G
CLIP = 1.0
LOG_2PI = np.log(2.0 * np.pi)
FMT = "e4m3"


def clip(v):
    return np.clip(v, -CLIP, CLIP)


def gaussian_multi(m1, v1, m2, v2):
    v1s = np.exp(2.0 * v1)
    v2s = np.exp(2.0 * v2)
    add = v1s + v2s
    log_add = np.log(add)
    scale = (-0.5 * (LOG_2PI + log_add + (m1 - m2) ** 2 / add)).sum(-1)
    mu = (m1 * v2s + m2 * v1s) / add
    var = v1 + v2 - 0.5 * log_add
    return scale, mu, var


def setup_inputs():
    s = mx_kscale(D)
    x = bf(np.random.standard_normal((B, P, D)) * s)
    s_weight = bf(np.random.standard_normal((B, P, NL, E)))
    s_mu = bf(clip(np.random.standard_normal((B, P, NL, E, G))))
    s_var = bf(clip(np.random.standard_normal((B, P, NL, E, G))))
    tcm_w_words, tcm_w_scales = pack_weight(np.random.standard_normal((D, WG)) / np.sqrt(D) / s[:, None], FMT)
    tcm_b = bf(np.random.standard_normal(WG) * 0.3)
    tcv_w_words, tcv_w_scales = pack_weight(np.random.standard_normal((D, WG)) / np.sqrt(D) / s[:, None], FMT)
    tcv_b = bf(np.random.standard_normal(WG) * 0.3)
    return {"x": x,
            "s_weight": s_weight,
            "s_mu": s_mu,
            "s_var": s_var,
            "tcm_w_words": tcm_w_words,
            "tcm_w_scales": tcm_w_scales,
            "tcm_b": tcm_b,
            "tcv_w_words": tcv_w_words,
            "tcv_w_scales": tcv_w_scales,
            "tcv_b": tcv_b}


def reference(x, s_weight, s_mu, s_var, tcm_w_words, tcm_w_scales, tcm_b, tcv_w_words, tcv_w_scales, tcv_b):
    xq = mxq(f64(x).reshape(B * P, D), 1, "e4m3")
    t_c_mu = clip(((xq @ unpack_weight(tcm_w_words, tcm_w_scales, FMT)) + f64(tcm_b)).reshape(B, P, NL, NL, T, G))[:, :, :, :, :, None, :]
    t_c_var = clip(((xq @ unpack_weight(tcv_w_words, tcv_w_scales, FMT)) + f64(tcv_b)).reshape(B, P, NL, NL, T, G))[:, :, :, :, :, None, :]
    m1 = f64(s_mu)[:, :, None, :, None, :, :]
    v1 = f64(s_var)[:, :, None, :, None, :, :]
    cs_scale, cs_mu, cs_var = gaussian_multi(m1, v1, t_c_mu, t_c_var)
    cs_scale = cs_scale + f64(s_weight)[:, :, None, :, None, :]
    return cs_scale, cs_mu, cs_var

@@ -1,0 +1,293 @@
+import math
+from contextlib import ExitStack
+
+import concourse.mybir as mybir
+from concourse.masks import make_identity
+
+F32 = mybir.dt.float32
+BF16 = mybir.dt.bfloat16
+I32 = mybir.dt.int32
+U32 = mybir.dt.uint32
+U8 = mybir.dt.uint8
+FP8X4 = mybir.dt.float8_e4m3fn_x4
+ALU = mybir.AluOpType
+ACT = mybir.ActivationFunctionType
+
+P = 128
+ROWS = 2 * 192
+ROW_TILES = ROWS // P
+K = 1024
+K_PASS = 4 * P
+PASSES = K // K_PASS
+LABELS = 16
+COMPONENTS = 2
+GAUSS = 2
+N = LABELS * LABELS * COMPONENTS * GAUSS
+BANK = 512
+HALVES = N // BANK
+STATE = LABELS * GAUSS
+TABLE = LABELS * COMPONENTS * GAUSS
+LOG_2PI = math.log(2.0 * math.pi)
+LOGSTD = 0
+MEAN = 1
+
+FLOPS = 2 * ROWS * K * 2 * N
+
+
+def tile_chainlveg_pa_kernel(
+    tc,
+    x,
+    s_weight,
+    s_mu,
+    s_var,
+    tcm_w_words,
+    tcm_w_scales,
+    tcm_b,
+    tcv_w_words,
+    tcv_w_scales,
+    tcv_b,
+    out_0,
+    out_1,
+    out_2,
+):
+    nc = tc.nc
+    words_in = [tcv_w_words, tcm_w_words]
+    scales_in = [tcv_w_scales, tcm_w_scales]
+    bias_in = [tcv_b, tcm_b]
+
+    x_view = x.flatten_outer_dims().rearrange("(r p) k -> p r k", p=P)
+    s_mu_view = s_mu.rearrange("b q j e g -> (b q) (j e g)").rearrange("(r p) c -> p r c", p=P)
+    s_var_view = s_var.rearrange("b q j e g -> (b q) (j e g)").rearrange("(r p) c -> p r c", p=P)
+    s_weight_view = s_weight.rearrange("b q j e -> (b q) (j e)").rearrange("(r p) c -> p r c", p=P)
+    scale_out = out_0.rearrange("b q i j t e -> (b q) (i j t e)")
+    mu_out = out_1.rearrange("b q i j t e g -> (b q) (i j t e g)")
+    var_out = out_2.rearrange("b q i j t e g -> (b q) (i j t e g)")
+
+    def cols(h):
+        return slice(h * BANK, (h + 1) * BANK)
+
+    def rows(r):
+        return slice(r * P, (r + 1) * P)
+
+    with ExitStack() as ctx:
+        keep = ctx.enter_context(tc.tile_pool(name="keep", bufs=1))
+        stage = ctx.enter_context(tc.tile_pool(name="stage", bufs=ROW_TILES))
+        xt_ps = ctx.enter_context(tc.psum_pool(name="xt_ps", bufs=2))
+        acc_ps = ctx.enter_context(tc.psum_pool(name="acc_ps", bufs=6))
+        ctx.enter_context(tc.manual_schedule())
+
+        x_sb = keep.tile([P, ROW_TILES, K], BF16)
+        ident = keep.tile([P, P], F32)
+        ones = keep.tile([P, P], BF16)
+        bias_rows = keep.tile([P, 2, N], BF16)
+        bias_all = keep.tile([P, 2, N], F32)
+        one_col = keep.tile([P, 1], F32)
+        two_col = keep.tile([P, 1], F32)
+        unused_col = keep.tile([P, 1], F32)
+        w_words = keep.tile([P, 2, PASSES, N], U32, align_bytes=64)
+        w_planes = [keep.tile([P, N], U8, name="w_planes%d" % w, align_bytes=64) for w in range(2)]
+        x_codes = keep.tile([P, ROW_TILES, PASSES * P], U32, align_bytes=64)
+        x_planes = keep.tile([P, ROW_TILES, PASSES * P], U8, align_bytes=64)
+        mu_in = keep.tile([P, ROW_TILES, STATE], BF16)
+        var_in = keep.tile([P, ROW_TILES, STATE], BF16)
+        weight_in = keep.tile([P, ROW_TILES, LABELS], BF16)
+        m1_tab = keep.tile([P, ROW_TILES, TABLE], F32)
+        v1_tab = keep.tile([P, ROW_TILES, TABLE], F32)
+        r1_small = keep.tile([P, ROW_TILES, STATE], F32)
+        r1_tab = keep.tile([P, ROW_TILES, TABLE], F32)
+        v_sum = keep.tile([P, ROW_TILES * LABELS], F32)
+        c_tab = keep.tile([P, ROW_TILES, LABELS * COMPONENTS], F32)
+
+        def per_row_tile(label, width):
+            return [keep.tile([P, width], F32, name="%s%d" % (label, r)) for r in range(ROW_TILES)]
+
+        proj = [per_row_tile("logstd", N), per_row_tile("mean", N)]
+        share = per_row_tile("share", N)
+        log_share = per_row_tile("log_share", N)
+        d_share = per_row_tile("d_share", N)
+        quad = per_row_tile("quad", N)
+        pair = per_row_tile("pair", N // GAUSS)
+
+        for w in range(2):
+            nc.vector.memset(w_planes[w][:].bitcast(I32), 0)
+        nc.vector.memset(bias_rows[:], 0.0)
+        nc.vector.memset(ones[:], 1.0)
+        nc.vector.memset(one_col[:], 1.0)
+        nc.vector.memset(two_col[:], 2.0)
+        make_identity(nc, ident[:])
+
+        for w in range(2):
+            nc.scalar.dma_start(out=bias_rows[0:1, w, :], in_=bias_in[w].unsqueeze(0))
+        nc.scalar.dma_start(out=var_in[:], in_=s_var_view)
+        nc.scalar.dma_start(out=mu_in[:], in_=s_mu_view)
+        nc.scalar.dma_start(out=weight_in[:], in_=s_weight_view)
+        nc.sync.dma_start(out=x_sb[:], in_=x_view)
+
+        def load_scales(w):
+            for quadrant in range(4):
+                nc.sync.dma_start(
+                    out=w_planes[w][32 * quadrant : 32 * quadrant + 4 * PASSES, :].bitcast(I32),
+                    in_=scales_in[w][:, 4 * quadrant : 4 * quadrant + 4, :].bitcast(I32),
+                )
+
+        def load_words(w, h):
+            by_partition = words_in[w].rearrange("g p n t -> p g (n t)")
+            nc.sync.dma_start(
+                out=w_words[:, w, :, cols(h)].bitcast(I32),
+                in_=by_partition[:, :, 4 * h * BANK : 4 * (h + 1) * BANK].bitcast(I32),
+            )
+
+        for w in (LOGSTD, MEAN):
+            load_scales(w)
+            for h in range(HALVES):
+                load_words(w, h)
+
+        def over_components(small):
+            pairs = small.rearrange("p r (j g) -> p (r j) g", g=GAUSS)
+            return pairs.unsqueeze(2).to_broadcast([P, ROW_TILES * LABELS, COMPONENTS, GAUSS])
+
+        def as_jtg(table):
+            return table.rearrange("p r (j t g) -> p (r j) t g", t=COMPONENTS, g=GAUSS)
+
+        nc.scalar.activation(out=r1_small[:], in_=var_in[:], func=ACT.Exp, scale=-2.0)
+        nc.scalar.activation(out=unused_col[:], in_=one_col[:], func=ACT.Sigmoid)
+
+        nc.vector.tensor_copy(out=as_jtg(m1_tab[:]), in_=over_components(mu_in[:]))
+        nc.vector.tensor_copy(out=as_jtg(v1_tab[:]), in_=over_components(var_in[:]))
+        var_pairs = var_in[:].rearrange("p r (j g) -> p (r j) g", g=GAUSS)
+        nc.vector.tensor_tensor(out=v_sum[:], in0=var_pairs[:, :, 0], in1=var_pairs[:, :, 1], op=ALU.add)
+        both = [P, ROW_TILES * LABELS, COMPONENTS]
+        nc.vector.scalar_tensor_tensor(
+            out=c_tab[:].rearrange("p r (j t) -> p (r j) t", t=COMPONENTS),
+            in0=weight_in[:].rearrange("p r j -> p (r j)").unsqueeze(2).to_broadcast(both),
+            scalar=LOG_2PI - 2.0,
+            in1=v_sum[:].unsqueeze(2).to_broadcast(both),
+            op0=ALU.subtract,
+            op1=ALU.subtract,
+        )
+        nc.vector.tensor_copy(out=as_jtg(r1_tab[:]), in_=over_components(r1_small[:]))
+
+        for w in (LOGSTD, MEAN):
+            for h in range(HALVES):
+                spread = acc_ps.tile([P, BANK], F32, name="spread", tag="acc")
+                nc.tensor.matmul(out=spread[:], lhsT=ones[:], rhs=bias_rows[:, w, cols(h)], start=True, stop=True)
+                nc.scalar.copy(out=bias_all[:, w, cols(h)], in_=spread[:])
+
+        x_words = x_sb[:].bitcast(F32)
+
+        def transpose_rows(r):
+            xt = xt_ps.tile([P, 2 * PASSES, P], F32, name="xt", tag="xt")
+            for g in range(PASSES):
+                for u in range(2):
+                    nc.tensor.transpose(
+                        xt[:, 2 * g + u, :], x_words[:, r, 256 * g + u : 256 * (g + 1) : 2], ident[:]
+                    )
+            return xt
+
+        def regroup(xt):
+            grouped = stage.tile([P, K], BF16, name="grouped", tag="grouped", align_bytes=64)
+            nc.vector.tensor_copy(
+                out=grouped[:].bitcast(F32).rearrange("p (g m u) -> p g m u", g=PASSES, u=2),
+                in_=xt[:].rearrange("p (g u) m -> p g m u", u=2),
+            )
+            return grouped
+
+        def quantise(r, grouped):
+            nc.vector.quantize_mx(
+                out=x_codes[:, r, :].bitcast(FP8X4), scales=x_planes[:, r, :], in_=grouped[:]
+            )
+
+        xt0 = transpose_rows(0)
+        xt1 = transpose_rows(1)
+        grouped0 = regroup(xt0)
+        xt2 = transpose_rows(2)
+        grouped1 = regroup(xt1)
+        quantise(0, grouped0)
+        grouped2 = regroup(xt2)
+        quantise(1, grouped1)
+        quantise(2, grouped2)
+
+        for w in (LOGSTD, MEAN):
+            for h in range(HALVES):
+                for r in range(ROW_TILES):
+                    acc = acc_ps.tile([P, BANK], F32, name="acc", tag="acc")
+                    for g in range(PASSES):
+                        nc.tensor.matmul_mx(
+                            out=acc[:],
+                            lhsT=x_codes[:, r, g * P : (g + 1) * P].bitcast(FP8X4),
+                            lhsT_scale=x_planes[:, r, g * P : (g + 1) * P],
+                            rhs=w_words[:, w, g, cols(h)].bitcast(FP8X4),
+                            rhs_scale=w_planes[w][4 * g : P, cols(h)],
+                            start=(g == 0),
+                            stop=(g == PASSES - 1),
+                        )
+                    nc.vector.tensor_tensor(
+                        out=proj[w][r][:, cols(h)], in0=acc[:], in1=bias_all[:, w, cols(h)], op=ALU.add
+                    )
+
+        def by_label(tile_ap, width):
+            return tile_ap.rearrange("p (i c) -> p i c", c=width)
+
+        def for_each_label(table, r, width):
+            return table[:, r, :].unsqueeze(1).to_broadcast([P, LABELS, width])
+
+        def clip_plus_one(t):
+            nc.scalar.activation(out=t[:], in_=t[:], func=ACT.Relu, bias=one_col[:], scale=-1.0)
+            nc.scalar.activation(out=t[:], in_=t[:], func=ACT.Relu, bias=two_col[:], scale=-1.0)
+
+        for r in range(ROW_TILES):
+            logstd, mean = proj[LOGSTD][r], proj[MEAN][r]
+            clip_plus_one(logstd)
+            clip_plus_one(mean)
+            nc.vector.scalar_tensor_tensor(
+                out=by_label(share[r][:], TABLE),
+                in0=by_label(logstd[:], TABLE),
+                scalar=1.0,
+                in1=for_each_label(v1_tab, r, TABLE),
+                op0=ALU.subtract,
+                op1=ALU.subtract,
+            )
+            nc.scalar.activation(out=share[r][:], in_=share[r][:], func=ACT.Sigmoid, scale=-2.0)
+            nc.vector.scalar_tensor_tensor(
+                out=by_label(mean[:], TABLE),
+                in0=by_label(mean[:], TABLE),
+                scalar=1.0,
+                in1=for_each_label(m1_tab, r, TABLE),
+                op0=ALU.subtract,
+                op1=ALU.subtract,
+            )
+            nc.vector.tensor_tensor(
+                out=by_label(quad[r][:], TABLE),
+                in0=by_label(mean[:], TABLE),
+                in1=for_each_label(r1_tab, r, TABLE),
+                op=ALU.mult,
+            )
+            nc.vector.tensor_tensor(out=d_share[r][:], in0=mean[:], in1=share[r][:], op=ALU.mult)
+            nc.vector.tensor_tensor(
+                out=by_label(mean[:], TABLE),
+                in0=by_label(d_share[r][:], TABLE),
+                in1=for_each_label(m1_tab, r, TABLE),
+                op=ALU.add,
+            )
+            nc.sync.dma_start(out=mu_out[rows(r), :], in_=mean[:])
+            nc.vector.tensor_tensor(out=quad[r][:], in0=quad[r][:], in1=d_share[r][:], op=ALU.mult)
+
+        for r in range(ROW_TILES):
+            logstd = proj[LOGSTD][r]
+            nc.scalar.activation(out=log_share[r][:], in_=share[r][:], func=ACT.Ln, scale=math.exp(-2.0))
+            nc.vector.scalar_tensor_tensor(
+                out=logstd[:], in0=log_share[r][:], scalar=0.5, in1=logstd[:], op0=ALU.mult, op1=ALU.add
+            )
+            nc.sync.dma_start(out=var_out[rows(r), :], in_=logstd[:])
+            nc.vector.tensor_tensor(out=quad[r][:], in0=quad[r][:], in1=log_share[r][:], op=ALU.subtract)
+            by_g = quad[r][:].rearrange("p (c g) -> p c g", g=GAUSS)
+            nc.vector.tensor_tensor(out=pair[r][:], in0=by_g[:, :, 0], in1=by_g[:, :, 1], op=ALU.add)
+            nc.vector.scalar_tensor_tensor(
+                out=by_label(pair[r][:], LABELS * COMPONENTS),
+                in0=by_label(pair[r][:], LABELS * COMPONENTS),
+                scalar=-0.5,
+                in1=for_each_label(c_tab, r, LABELS * COMPONENTS),
+                op0=ALU.mult,
+                op1=ALU.add,
+            )
+            nc.sync.dma_start(out=scale_out[rows(r), :], in_=pair[r][:])

@@ -23,8 +23,9 @@ LABELS = 16
 COMPONENTS = 2
 GAUSS = 2
 N = LABELS * LABELS * COMPONENTS * GAUSS
-BANK = 512
-HALVES = N // BANK
+BLOCKS = N // P
+GROUP = 4
+GROUPS = BLOCKS // GROUP
 STATE = LABELS * GAUSS
 TABLE = LABELS * COMPONENTS * GAUSS
 LOG_2PI = math.log(2.0 * math.pi)
@@ -55,39 +56,46 @@ def tile_chainlveg_pa_kernel(
     scales_in = [tcv_w_scales, tcm_w_scales]
     bias_in = [tcv_b, tcm_b]
 
-    x_view = x.flatten_outer_dims().rearrange("(r p) k -> p r k", p=P)
-    s_mu_view = s_mu.rearrange("b q j e g -> (b q) (j e g)").rearrange("(r p) c -> p r c", p=P)
-    s_var_view = s_var.rearrange("b q j e g -> (b q) (j e g)").rearrange("(r p) c -> p r c", p=P)
-    s_weight_view = s_weight.rearrange("b q j e -> (b q) (j e)").rearrange("(r p) c -> p r c", p=P)
-    scale_out = out_0.rearrange("b q i j t e -> (b q) (i j t e)")
-    mu_out = out_1.rearrange("b q i j t e g -> (b q) (i j t e g)")
-    var_out = out_2.rearrange("b q i j t e g -> (b q) (i j t e g)")
+    def by_row_tile(flat):
+        return flat.rearrange("(r p) c -> p r c", p=P)
 
-    def cols(h):
-        return slice(h * BANK, (h + 1) * BANK)
+    x_view = by_row_tile(x.flatten_outer_dims())
+    s_mu_view = by_row_tile(s_mu.rearrange("b q j e g -> (b q) (j e g)"))
+    s_var_view = by_row_tile(s_var.rearrange("b q j e g -> (b q) (j e g)"))
+    s_weight_view = by_row_tile(s_weight.rearrange("b q j e -> (b q) (j e)"))
+    scale_out = by_row_tile(out_0.rearrange("b q i j t e -> (b q) (i j t e)"))
+    mu_out = by_row_tile(out_1.rearrange("b q i j t e g -> (b q) (i j t e g)"))
+    var_out = by_row_tile(out_2.rearrange("b q i j t e g -> (b q) (i j t e g)"))
 
     def rows(r):
         return slice(r * P, (r + 1) * P)
 
+    def blocks(h):
+        return slice(h * GROUP, (h + 1) * GROUP)
+
+    def columns(h, per_block):
+        return slice(h * GROUP * per_block, (h + 1) * GROUP * per_block)
+
     with ExitStack() as ctx:
         keep = ctx.enter_context(tc.tile_pool(name="keep", bufs=1))
         stage = ctx.enter_context(tc.tile_pool(name="stage", bufs=ROW_TILES))
-        xt_ps = ctx.enter_context(tc.psum_pool(name="xt_ps", bufs=2))
-        acc_ps = ctx.enter_context(tc.psum_pool(name="acc_ps", bufs=6))
+        tab_ps = ctx.enter_context(tc.psum_pool(name="tab_ps", bufs=1))
+        bank_ps = ctx.enter_context(tc.psum_pool(name="bank_ps", bufs=5))
         ctx.enter_context(tc.manual_schedule())
 
         x_sb = keep.tile([P, ROW_TILES, K], BF16)
         ident = keep.tile([P, P], F32)
-        ones = keep.tile([P, P], BF16)
-        bias_rows = keep.tile([P, 2, N], BF16)
-        bias_all = keep.tile([P, 2, N], F32)
+        pair_pos = keep.tile([P, P // GAUSS], F32)
+        pair_neg = keep.tile([P, P // GAUSS], F32)
+        bias_rows = keep.tile([P, P], BF16)
+        bias_rows_f32 = keep.tile([P, P], F32)
+        one_minus_bias = keep.tile([P, 2 * BLOCKS], F32)
         one_col = keep.tile([P, 1], F32)
-        two_col = keep.tile([P, 1], F32)
         unused_col = keep.tile([P, 1], F32)
         w_words = keep.tile([P, 2, PASSES, N], U32, align_bytes=64)
         w_planes = [keep.tile([P, N], U8, name="w_planes%d" % w, align_bytes=64) for w in range(2)]
-        x_codes = keep.tile([P, ROW_TILES, PASSES * P], U32, align_bytes=64)
-        x_planes = keep.tile([P, ROW_TILES, PASSES * P], U8, align_bytes=64)
+        x_codes = keep.tile([P, PASSES, ROWS], U32, align_bytes=64)
+        x_planes = keep.tile([P, PASSES, ROWS], U8, align_bytes=64)
         mu_in = keep.tile([P, ROW_TILES, STATE], BF16)
         var_in = keep.tile([P, ROW_TILES, STATE], BF16)
         weight_in = keep.tile([P, ROW_TILES, LABELS], BF16)
@@ -97,31 +105,39 @@ def tile_chainlveg_pa_kernel(
         r1_tab = keep.tile([P, ROW_TILES, TABLE], F32)
         v_sum = keep.tile([P, ROW_TILES * LABELS], F32)
         c_tab = keep.tile([P, ROW_TILES, LABELS * COMPONENTS], F32)
+        wide_v1 = keep.tile([P, ROW_TILES, P], F32)
+        wide_m1 = keep.tile([P, ROW_TILES, P], F32)
+        wide_r1 = keep.tile([P, ROW_TILES, P], F32)
+        one_minus_v1 = tab_ps.tile([P, ROWS], F32)
+        one_minus_m1 = tab_ps.tile([P, ROWS], F32)
+        inv_e1 = tab_ps.tile([P, ROWS], F32)
 
-        def per_row_tile(label, width):
-            return [keep.tile([P, width], F32, name="%s%d" % (label, r)) for r in range(ROW_TILES)]
-
-        proj = [per_row_tile("logstd", N), per_row_tile("mean", N)]
-        share = per_row_tile("share", N)
-        log_share = per_row_tile("log_share", N)
-        d_share = per_row_tile("d_share", N)
-        quad = per_row_tile("quad", N)
-        pair = per_row_tile("pair", N // GAUSS)
+        clipped = [keep.tile([P, BLOCKS, ROWS], F32, name="clipped%d" % w) for w in range(2)]
+        share = clipped[LOGSTD]
+        gap = clipped[MEAN]
+        quad = keep.tile([P, BLOCKS, ROWS], F32)
+        gap_share = keep.tile([P, BLOCKS, ROWS], F32)
+        log_share = keep.tile([P, BLOCKS, ROWS], F32)
+        log_rest = keep.tile([P, BLOCKS, ROWS], F32)
+        mu_sb = keep.tile([P, ROW_TILES, N], F32)
+        var_sb = keep.tile([P, ROW_TILES, N], F32)
+        scale_sb = keep.tile([P, ROW_TILES, N // GAUSS], F32)
 
         for w in range(2):
             nc.vector.memset(w_planes[w][:].bitcast(I32), 0)
         nc.vector.memset(bias_rows[:], 0.0)
-        nc.vector.memset(ones[:], 1.0)
         nc.vector.memset(one_col[:], 1.0)
-        nc.vector.memset(two_col[:], 2.0)
         make_identity(nc, ident[:])
 
-        for w in range(2):
-            nc.scalar.dma_start(out=bias_rows[0:1, w, :], in_=bias_in[w].unsqueeze(0))
+        nc.sync.dma_start(out=x_sb[:], in_=x_view)
         nc.scalar.dma_start(out=var_in[:], in_=s_var_view)
         nc.scalar.dma_start(out=mu_in[:], in_=s_mu_view)
-        nc.scalar.dma_start(out=weight_in[:], in_=s_weight_view)
-        nc.sync.dma_start(out=x_sb[:], in_=x_view)
+        for w in (LOGSTD, MEAN):
+            nc.gpsimd.dma_start(
+                out=bias_rows[w * BLOCKS : (w + 1) * BLOCKS, :],
+                in_=bias_in[w].rearrange("(b c) -> b c", c=P),
+            )
+        nc.gpsimd.dma_start(out=weight_in[:], in_=s_weight_view)
 
         def load_scales(w):
             for quadrant in range(4):
@@ -133,50 +149,21 @@ def tile_chainlveg_pa_kernel(
         def load_words(w, h):
             by_partition = words_in[w].rearrange("g p n t -> p g (n t)")
             nc.sync.dma_start(
-                out=w_words[:, w, :, cols(h)].bitcast(I32),
-                in_=by_partition[:, :, 4 * h * BANK : 4 * (h + 1) * BANK].bitcast(I32),
+                out=w_words[:, w, :, columns(h, P)].bitcast(I32),
+                in_=by_partition[:, :, columns(h, 4 * P)].bitcast(I32),
             )
 
-        for w in (LOGSTD, MEAN):
-            load_scales(w)
-            for h in range(HALVES):
-                load_words(w, h)
-
-        def over_components(small):
-            pairs = small.rearrange("p r (j g) -> p (r j) g", g=GAUSS)
-            return pairs.unsqueeze(2).to_broadcast([P, ROW_TILES * LABELS, COMPONENTS, GAUSS])
-
-        def as_jtg(table):
-            return table.rearrange("p r (j t g) -> p (r j) t g", t=COMPONENTS, g=GAUSS)
-
-        nc.scalar.activation(out=r1_small[:], in_=var_in[:], func=ACT.Exp, scale=-2.0)
-        nc.scalar.activation(out=unused_col[:], in_=one_col[:], func=ACT.Sigmoid)
-
-        nc.vector.tensor_copy(out=as_jtg(m1_tab[:]), in_=over_components(mu_in[:]))
-        nc.vector.tensor_copy(out=as_jtg(v1_tab[:]), in_=over_components(var_in[:]))
-        var_pairs = var_in[:].rearrange("p r (j g) -> p (r j) g", g=GAUSS)
-        nc.vector.tensor_tensor(out=v_sum[:], in0=var_pairs[:, :, 0], in1=var_pairs[:, :, 1], op=ALU.add)
-        both = [P, ROW_TILES * LABELS, COMPONENTS]
-        nc.vector.scalar_tensor_tensor(
-            out=c_tab[:].rearrange("p r (j t) -> p (r j) t", t=COMPONENTS),
-            in0=weight_in[:].rearrange("p r j -> p (r j)").unsqueeze(2).to_broadcast(both),
-            scalar=LOG_2PI - 2.0,
-            in1=v_sum[:].unsqueeze(2).to_broadcast(both),
-            op0=ALU.subtract,
-            op1=ALU.subtract,
-        )
-        nc.vector.tensor_copy(out=as_jtg(r1_tab[:]), in_=over_components(r1_small[:]))
-
-        for w in (LOGSTD, MEAN):
-            for h in range(HALVES):
-                spread = acc_ps.tile([P, BANK], F32, name="spread", tag="acc")
-                nc.tensor.matmul(out=spread[:], lhsT=ones[:], rhs=bias_rows[:, w, cols(h)], start=True, stop=True)
-                nc.scalar.copy(out=bias_all[:, w, cols(h)], in_=spread[:])
+        load_scales(LOGSTD)
+        load_words(LOGSTD, 0)
+        load_words(MEAN, 0)
+        load_scales(MEAN)
+        load_words(LOGSTD, 1)
+        load_words(MEAN, 1)
 
         x_words = x_sb[:].bitcast(F32)
 
         def transpose_rows(r):
-            xt = xt_ps.tile([P, 2 * PASSES, P], F32, name="xt", tag="xt")
+            xt = bank_ps.tile([P, 2 * PASSES, P], F32, name="xt", tag="bank")
             for g in range(PASSES):
                 for u in range(2):
                     nc.tensor.transpose(
@@ -193,101 +180,201 @@ def tile_chainlveg_pa_kernel(
             return grouped
 
         def quantise(r, grouped):
-            nc.vector.quantize_mx(
-                out=x_codes[:, r, :].bitcast(FP8X4), scales=x_planes[:, r, :], in_=grouped[:]
-            )
+            for g in range(PASSES):
+                nc.vector.quantize_mx(
+                    out=x_codes[:, g, rows(r)].bitcast(FP8X4),
+                    scales=x_planes[:, g, rows(r)],
+                    in_=grouped[:, g * K_PASS : (g + 1) * K_PASS],
+                )
 
         xt0 = transpose_rows(0)
         xt1 = transpose_rows(1)
-        grouped0 = regroup(xt0)
         xt2 = transpose_rows(2)
+        grouped0 = regroup(xt0)
+        nc.vector.tensor_copy(out=bias_rows_f32[:], in_=bias_rows[:])
+        bias_cols = bank_ps.tile([P, P], F32, name="bias_cols", tag="bank")
+        nc.tensor.transpose(bias_cols[:], bias_rows_f32[:], ident[:])
         grouped1 = regroup(xt1)
         quantise(0, grouped0)
         grouped2 = regroup(xt2)
         quantise(1, grouped1)
+        nc.vector.tensor_scalar(
+            out=one_minus_bias[:],
+            in0=bias_cols[:, 0 : 2 * BLOCKS],
+            scalar1=-1.0,
+            scalar2=1.0,
+            op0=ALU.mult,
+            op1=ALU.add,
+        )
         quantise(2, grouped2)
 
-        for w in (LOGSTD, MEAN):
-            for h in range(HALVES):
-                for r in range(ROW_TILES):
-                    acc = acc_ps.tile([P, BANK], F32, name="acc", tag="acc")
-                    for g in range(PASSES):
-                        nc.tensor.matmul_mx(
-                            out=acc[:],
-                            lhsT=x_codes[:, r, g * P : (g + 1) * P].bitcast(FP8X4),
-                            lhsT_scale=x_planes[:, r, g * P : (g + 1) * P],
-                            rhs=w_words[:, w, g, cols(h)].bitcast(FP8X4),
-                            rhs_scale=w_planes[w][4 * g : P, cols(h)],
-                            start=(g == 0),
-                            stop=(g == PASSES - 1),
-                        )
-                    nc.vector.tensor_tensor(
-                        out=proj[w][r][:, cols(h)], in0=acc[:], in1=bias_all[:, w, cols(h)], op=ALU.add
-                    )
+        def over_components(small):
+            pairs = small.rearrange("p r (j g) -> p (r j) g", g=GAUSS)
+            return pairs.unsqueeze(2).to_broadcast([P, ROW_TILES * LABELS, COMPONENTS, GAUSS])
 
-        def by_label(tile_ap, width):
-            return tile_ap.rearrange("p (i c) -> p i c", c=width)
+        def as_jtg(table):
+            return table.rearrange("p r (j t g) -> p (r j) t g", t=COMPONENTS, g=GAUSS)
+
+        def twice(table):
+            return table.unsqueeze(2).to_broadcast([P, ROW_TILES, P // TABLE, TABLE])
+
+        def as_two(wide):
+            return wide.rearrange("p r (i c) -> p r i c", c=TABLE)
+
+        def transpose_table(table_ps, wide):
+            for r in range(ROW_TILES):
+                nc.tensor.transpose(table_ps[:, rows(r)], wide[:, r, :], ident[:])
+
+        nc.scalar.activation(out=r1_small[:], in_=var_in[:], func=ACT.Exp, scale=-2.0)
+        nc.scalar.activation(out=unused_col[:], in_=one_col[:], func=ACT.Sigmoid)
+
+        nc.vector.tensor_copy(out=as_jtg(v1_tab[:]), in_=over_components(var_in[:]))
+        nc.vector.tensor_scalar(
+            out=as_two(wide_v1[:]), in0=twice(v1_tab[:]), scalar1=-1.0, scalar2=1.0, op0=ALU.mult, op1=ALU.add
+        )
+        nc.vector.tensor_copy(out=as_jtg(m1_tab[:]), in_=over_components(mu_in[:]))
+        nc.vector.tensor_scalar(
+            out=as_two(wide_m1[:]), in0=twice(m1_tab[:]), scalar1=-1.0, scalar2=1.0, op0=ALU.mult, op1=ALU.add
+        )
+        nc.vector.tensor_copy(out=as_jtg(r1_tab[:]), in_=over_components(r1_small[:]))
+        nc.vector.tensor_copy(out=as_two(wide_r1[:]), in_=twice(r1_tab[:]))
+        ident_pairs = ident[:].rearrange("p (k g) -> p k g", g=GAUSS)
+        nc.vector.tensor_tensor(out=pair_pos[:], in0=ident_pairs[:, :, 0], in1=ident_pairs[:, :, 1], op=ALU.add)
+        nc.vector.tensor_scalar_mul(out=pair_neg[:], in0=pair_pos[:], scalar1=-1.0)
+
+        def project(w, b):
+            acc = bank_ps.tile([P, ROWS], F32, name="acc", tag="bank")
+            for moving in (slice(0, 2 * P), slice(2 * P, ROWS)):
+                for g in range(PASSES):
+                    nc.tensor.matmul_mx(
+                        out=acc[:, moving],
+                        lhsT=w_words[:, w, g, b * P : (b + 1) * P].bitcast(FP8X4),
+                        lhsT_scale=w_planes[w][4 * g : P, b * P : (b + 1) * P],
+                        rhs=x_codes[:, g, moving].bitcast(FP8X4),
+                        rhs_scale=x_planes[:, g, moving],
+                        start=(g == 0),
+                        stop=(g == PASSES - 1),
+                    )
+            nc.scalar.activation(
+                out=clipped[w][:, b, :],
+                in_=acc[:],
+                func=ACT.Relu,
+                bias=one_minus_bias[:, w * BLOCKS + b : w * BLOCKS + b + 1],
+                scale=-1.0,
+            )
+
+        def project_group(w, h):
+            for b in range(h * GROUP, (h + 1) * GROUP):
+                project(w, b)
+
+        def for_each_block(table_ps):
+            return table_ps[:].unsqueeze(1).to_broadcast([P, GROUP, ROWS])
+
+        def lower_clip_minus(t, h, table_ps):
+            nc.vector.scalar_tensor_tensor(
+                out=t[:, blocks(h), :],
+                in0=t[:, blocks(h), :],
+                scalar=2.0,
+                in1=for_each_block(table_ps),
+                op0=ALU.min,
+                op1=ALU.subtract,
+            )
+
+        def share_of(h):
+            lower_clip_minus(share, h, one_minus_v1)
+            nc.scalar.activation(out=share[:, blocks(h), :], in_=share[:, blocks(h), :], func=ACT.Sigmoid, scale=2.0)
+
+        def gap_of(h):
+            lower_clip_minus(gap, h, one_minus_m1)
+            nc.vector.tensor_tensor(
+                out=quad[:, blocks(h), :], in0=gap[:, blocks(h), :], in1=for_each_block(inv_e1), op=ALU.mult
+            )
+
+        def to_rows(src, h, r):
+            back = bank_ps.tile([P, GROUP, P], F32, name="back", tag="bank")
+            for k in range(GROUP):
+                nc.tensor.transpose(back[:, k, :], src[:, h * GROUP + k, rows(r)], ident[:])
+            return back
+
+        def by_label(ap, width):
+            return ap.rearrange("p (i c) -> p i c", c=width)
 
         def for_each_label(table, r, width):
-            return table[:, r, :].unsqueeze(1).to_broadcast([P, LABELS, width])
+            return table[:, r, :].unsqueeze(1).to_broadcast([P, LABELS // GROUPS, width])
 
-        def clip_plus_one(t):
-            nc.scalar.activation(out=t[:], in_=t[:], func=ACT.Relu, bias=one_col[:], scale=-1.0)
-            nc.scalar.activation(out=t[:], in_=t[:], func=ACT.Relu, bias=two_col[:], scale=-1.0)
-
-        for r in range(ROW_TILES):
-            logstd, mean = proj[LOGSTD][r], proj[MEAN][r]
-            clip_plus_one(logstd)
-            clip_plus_one(mean)
-            nc.vector.scalar_tensor_tensor(
-                out=by_label(share[r][:], TABLE),
-                in0=by_label(logstd[:], TABLE),
-                scalar=1.0,
-                in1=for_each_label(v1_tab, r, TABLE),
-                op0=ALU.subtract,
-                op1=ALU.subtract,
-            )
-            nc.scalar.activation(out=share[r][:], in_=share[r][:], func=ACT.Sigmoid, scale=-2.0)
-            nc.vector.scalar_tensor_tensor(
-                out=by_label(mean[:], TABLE),
-                in0=by_label(mean[:], TABLE),
-                scalar=1.0,
-                in1=for_each_label(m1_tab, r, TABLE),
-                op0=ALU.subtract,
-                op1=ALU.subtract,
+        def products_and_mu(h):
+            nc.vector.tensor_tensor(
+                out=gap_share[:, blocks(h), :], in0=gap[:, blocks(h), :], in1=share[:, blocks(h), :], op=ALU.mult
             )
             nc.vector.tensor_tensor(
-                out=by_label(quad[r][:], TABLE),
-                in0=by_label(mean[:], TABLE),
-                in1=for_each_label(r1_tab, r, TABLE),
-                op=ALU.mult,
+                out=quad[:, blocks(h), :], in0=quad[:, blocks(h), :], in1=gap_share[:, blocks(h), :], op=ALU.mult
             )
-            nc.vector.tensor_tensor(out=d_share[r][:], in0=mean[:], in1=share[r][:], op=ALU.mult)
-            nc.vector.tensor_tensor(
-                out=by_label(mean[:], TABLE),
-                in0=by_label(d_share[r][:], TABLE),
-                in1=for_each_label(m1_tab, r, TABLE),
-                op=ALU.add,
-            )
-            nc.sync.dma_start(out=mu_out[rows(r), :], in_=mean[:])
-            nc.vector.tensor_tensor(out=quad[r][:], in0=quad[r][:], in1=d_share[r][:], op=ALU.mult)
+            for r in range(ROW_TILES):
+                back = to_rows(gap_share, h, r)
+                nc.vector.tensor_tensor(
+                    out=by_label(mu_sb[:, r, columns(h, P)], TABLE),
+                    in0=for_each_label(m1_tab, r, TABLE),
+                    in1=back[:].rearrange("p k (i c) -> p (k i) c", c=TABLE),
+                    op=ALU.subtract,
+                )
+            nc.sync.dma_start(out=mu_out[:, :, columns(h, P)], in_=mu_sb[:, :, columns(h, P)])
 
-        for r in range(ROW_TILES):
-            logstd = proj[LOGSTD][r]
-            nc.scalar.activation(out=log_share[r][:], in_=share[r][:], func=ACT.Ln, scale=math.exp(-2.0))
-            nc.vector.scalar_tensor_tensor(
-                out=logstd[:], in0=log_share[r][:], scalar=0.5, in1=logstd[:], op0=ALU.mult, op1=ALU.add
+        project_group(LOGSTD, 0)
+        transpose_table(one_minus_v1, wide_v1)
+        project_group(MEAN, 0)
+        transpose_table(one_minus_m1, wide_m1)
+        transpose_table(inv_e1, wide_r1)
+        share_of(0)
+        gap_of(0)
+        var_pairs = var_in[:].rearrange("p r (j g) -> p (r j) g", g=GAUSS)
+        nc.vector.tensor_tensor(out=v_sum[:], in0=var_pairs[:, :, 0], in1=var_pairs[:, :, 1], op=ALU.add)
+        both = [P, ROW_TILES * LABELS, COMPONENTS]
+        nc.vector.scalar_tensor_tensor(
+            out=c_tab[:].rearrange("p r (j t) -> p (r j) t", t=COMPONENTS),
+            in0=weight_in[:].rearrange("p r j -> p (r j)").unsqueeze(2).to_broadcast(both),
+            scalar=LOG_2PI,
+            in1=v_sum[:].unsqueeze(2).to_broadcast(both),
+            op0=ALU.subtract,
+            op1=ALU.subtract,
+        )
+        project_group(LOGSTD, 1)
+        project_group(MEAN, 1)
+        share_of(1)
+        products_and_mu(0)
+        gap_of(1)
+        products_and_mu(1)
+
+        for h in range(GROUPS):
+            nc.scalar.activation(out=log_share[:, blocks(h), :], in_=share[:, blocks(h), :], func=ACT.Ln)
+            nc.scalar.activation(
+                out=log_rest[:, blocks(h), :], in_=share[:, blocks(h), :], func=ACT.Ln, bias=one_col[:], scale=-1.0
             )
-            nc.sync.dma_start(out=var_out[rows(r), :], in_=logstd[:])
-            nc.vector.tensor_tensor(out=quad[r][:], in0=quad[r][:], in1=log_share[r][:], op=ALU.subtract)
-            by_g = quad[r][:].rearrange("p (c g) -> p c g", g=GAUSS)
-            nc.vector.tensor_tensor(out=pair[r][:], in0=by_g[:, :, 0], in1=by_g[:, :, 1], op=ALU.add)
-            nc.vector.scalar_tensor_tensor(
-                out=by_label(pair[r][:], LABELS * COMPONENTS),
-                in0=by_label(pair[r][:], LABELS * COMPONENTS),
-                scalar=-0.5,
-                in1=for_each_label(c_tab, r, LABELS * COMPONENTS),
-                op0=ALU.mult,
-                op1=ALU.add,
+        for h in range(GROUPS):
+            for r in range(ROW_TILES):
+                back = to_rows(log_rest, h, r)
+                nc.vector.scalar_tensor_tensor(
+                    out=by_label(var_sb[:, r, columns(h, P)], TABLE),
+                    in0=back[:].rearrange("p k (i c) -> p (k i) c", c=TABLE),
+                    scalar=0.5,
+                    in1=for_each_label(v1_tab, r, TABLE),
+                    op0=ALU.mult,
+                    op1=ALU.add,
+                )
+            nc.sync.dma_start(out=var_out[:, :, columns(h, P)], in_=var_sb[:, :, columns(h, P)])
+            for r in range(ROW_TILES):
+                sums = bank_ps.tile([P, GROUP, P // GAUSS], F32, name="sums", tag="bank")
+                for k in range(GROUP):
+                    b = h * GROUP + k
+                    nc.tensor.matmul(out=sums[:, k, :], lhsT=log_share[:, b, rows(r)], rhs=pair_neg[:], start=True, stop=False)
+                    nc.tensor.matmul(out=sums[:, k, :], lhsT=quad[:, b, rows(r)], rhs=pair_pos[:], start=False, stop=True)
+                nc.vector.scalar_tensor_tensor(
+                    out=by_label(scale_sb[:, r, columns(h, P // GAUSS)], LABELS * COMPONENTS),
+                    in0=sums[:].rearrange("p k (i c) -> p (k i) c", c=LABELS * COMPONENTS),
+                    scalar=-0.5,
+                    in1=for_each_label(c_tab, r, LABELS * COMPONENTS),
+                    op0=ALU.mult,
+                    op1=ALU.add,
+                )
+            nc.sync.dma_start(
+                out=scale_out[:, :, columns(h, P // GAUSS)], in_=scale_sb[:, :, columns(h, P // GAUSS)]
             )
-            nc.sync.dma_start(out=scale_out[rows(r), :], in_=pair[r][:])

@@ -23,11 +23,11 @@ LABELS = 16
 COMPONENTS = 2
 GAUSS = 2
 N = LABELS * LABELS * COMPONENTS * GAUSS
-BLOCKS = N // P
-GROUP = 4
-GROUPS = BLOCKS // GROUP
+BANK = 512
+HALVES = N // BANK
 STATE = LABELS * GAUSS
 TABLE = LABELS * COMPONENTS * GAUSS
+HALF_TABLE = LABELS * COMPONENTS
 LOG_2PI = math.log(2.0 * math.pi)
 LOGSTD = 0
 MEAN = 1
@@ -67,77 +67,57 @@ def tile_chainlveg_pa_kernel(
     mu_out = by_row_tile(out_1.rearrange("b q i j t e g -> (b q) (i j t e g)"))
     var_out = by_row_tile(out_2.rearrange("b q i j t e g -> (b q) (i j t e g)"))
 
-    def rows(r):
-        return slice(r * P, (r + 1) * P)
-
-    def blocks(h):
-        return slice(h * GROUP, (h + 1) * GROUP)
-
-    def columns(h, per_block):
-        return slice(h * GROUP * per_block, (h + 1) * GROUP * per_block)
+    def cols(h):
+        return slice(h * BANK, (h + 1) * BANK)
 
     with ExitStack() as ctx:
         keep = ctx.enter_context(tc.tile_pool(name="keep", bufs=1))
         stage = ctx.enter_context(tc.tile_pool(name="stage", bufs=ROW_TILES))
         tab_ps = ctx.enter_context(tc.psum_pool(name="tab_ps", bufs=1))
-        bank_ps = ctx.enter_context(tc.psum_pool(name="bank_ps", bufs=5))
+        bank_ps = ctx.enter_context(tc.psum_pool(name="bank_ps", bufs=6))
         ctx.enter_context(tc.manual_schedule())
 
         x_sb = keep.tile([P, ROW_TILES, K], BF16)
         ident = keep.tile([P, P], F32)
-        pair_pos = keep.tile([P, P // GAUSS], F32)
-        pair_neg = keep.tile([P, P // GAUSS], F32)
-        bias_rows = keep.tile([P, P], BF16)
-        bias_rows_f32 = keep.tile([P, P], F32)
-        one_minus_bias = keep.tile([P, 2 * BLOCKS], F32)
+        ones = keep.tile([P, P], BF16)
+        bias_rows = keep.tile([P, 2, N], BF16)
+        bias_all = keep.tile([P, 2, N], F32)
         one_col = keep.tile([P, 1], F32)
         unused_col = keep.tile([P, 1], F32)
         w_words = keep.tile([P, 2, PASSES, N], U32, align_bytes=64)
         w_planes = [keep.tile([P, N], U8, name="w_planes%d" % w, align_bytes=64) for w in range(2)]
-        x_codes = keep.tile([P, PASSES, ROWS], U32, align_bytes=64)
-        x_planes = keep.tile([P, PASSES, ROWS], U8, align_bytes=64)
+        x_codes = keep.tile([P, ROW_TILES, PASSES * P], U32, align_bytes=64)
+        x_planes = keep.tile([P, ROW_TILES, PASSES * P], U8, align_bytes=64)
         mu_in = keep.tile([P, ROW_TILES, STATE], BF16)
         var_in = keep.tile([P, ROW_TILES, STATE], BF16)
         weight_in = keep.tile([P, ROW_TILES, LABELS], BF16)
-        m1_tab = keep.tile([P, ROW_TILES, TABLE], F32)
-        v1_tab = keep.tile([P, ROW_TILES, TABLE], F32)
-        r1_small = keep.tile([P, ROW_TILES, STATE], F32)
-        r1_tab = keep.tile([P, ROW_TILES, TABLE], F32)
         v_sum = keep.tile([P, ROW_TILES * LABELS], F32)
-        c_tab = keep.tile([P, ROW_TILES, LABELS * COMPONENTS], F32)
-        wide_v1 = keep.tile([P, ROW_TILES, P], F32)
-        wide_m1 = keep.tile([P, ROW_TILES, P], F32)
-        wide_r1 = keep.tile([P, ROW_TILES, P], F32)
-        one_minus_v1 = tab_ps.tile([P, ROWS], F32)
-        one_minus_m1 = tab_ps.tile([P, ROWS], F32)
-        inv_e1 = tab_ps.tile([P, ROWS], F32)
+        plus_one_sb = keep.tile([P, 2, ROW_TILES, TABLE], F32)
+        inv_e1_sb = keep.tile([P, ROW_TILES, TABLE], F32)
+        v1_sb = keep.tile([P, ROW_TILES, TABLE], F32)
+        c_sb = keep.tile([P, ROW_TILES, HALF_TABLE], F32)
+        plus_one = tab_ps.tile([P, 2, ROW_TILES, TABLE], F32)
+        others = tab_ps.tile([P, 2 * ROW_TILES * TABLE + ROW_TILES * HALF_TABLE], F32)
+        inv_e1 = others[:, 0 : ROW_TILES * TABLE].rearrange("p (r c) -> p r c", c=TABLE)
+        v1_tab = others[:, ROW_TILES * TABLE : 2 * ROW_TILES * TABLE].rearrange("p (r c) -> p r c", c=TABLE)
+        c_tab = others[:, 2 * ROW_TILES * TABLE :].rearrange("p (r c) -> p r c", c=HALF_TABLE)
 
-        clipped = [keep.tile([P, BLOCKS, ROWS], F32, name="clipped%d" % w) for w in range(2)]
-        share = clipped[LOGSTD]
-        gap = clipped[MEAN]
-        quad = keep.tile([P, BLOCKS, ROWS], F32)
-        gap_share = keep.tile([P, BLOCKS, ROWS], F32)
-        log_share = keep.tile([P, BLOCKS, ROWS], F32)
-        log_rest = keep.tile([P, BLOCKS, ROWS], F32)
-        mu_sb = keep.tile([P, ROW_TILES, N], F32)
-        var_sb = keep.tile([P, ROW_TILES, N], F32)
-        scale_sb = keep.tile([P, ROW_TILES, N // GAUSS], F32)
+        def per_row_tile(label, width):
+            return [keep.tile([P, width], F32, name="%s%d" % (label, r)) for r in range(ROW_TILES)]
+
+        proj = [per_row_tile("logstd", N), per_row_tile("mean", N)]
+        d_share = per_row_tile("d_share", N)
+        quad = per_row_tile("quad", N)
+        log_share = per_row_tile("log_share", N)
+        log_rest = per_row_tile("log_rest", N)
+        pair = per_row_tile("pair", N // GAUSS)
 
         for w in range(2):
             nc.vector.memset(w_planes[w][:].bitcast(I32), 0)
         nc.vector.memset(bias_rows[:], 0.0)
+        nc.vector.memset(ones[:], 1.0)
         nc.vector.memset(one_col[:], 1.0)
         make_identity(nc, ident[:])
-
-        nc.sync.dma_start(out=x_sb[:], in_=x_view)
-        nc.scalar.dma_start(out=var_in[:], in_=s_var_view)
-        nc.scalar.dma_start(out=mu_in[:], in_=s_mu_view)
-        for w in (LOGSTD, MEAN):
-            nc.gpsimd.dma_start(
-                out=bias_rows[w * BLOCKS : (w + 1) * BLOCKS, :],
-                in_=bias_in[w].rearrange("(b c) -> b c", c=P),
-            )
-        nc.gpsimd.dma_start(out=weight_in[:], in_=s_weight_view)
 
         def load_scales(w):
             for quadrant in range(4):
@@ -149,16 +129,50 @@ def tile_chainlveg_pa_kernel(
         def load_words(w, h):
             by_partition = words_in[w].rearrange("g p n t -> p g (n t)")
             nc.sync.dma_start(
-                out=w_words[:, w, :, columns(h, P)].bitcast(I32),
-                in_=by_partition[:, :, columns(h, 4 * P)].bitcast(I32),
+                out=w_words[:, w, :, cols(h)].bitcast(I32),
+                in_=by_partition[:, :, 4 * h * BANK : 4 * (h + 1) * BANK].bitcast(I32),
             )
 
-        load_scales(LOGSTD)
-        load_words(LOGSTD, 0)
-        load_words(MEAN, 0)
-        load_scales(MEAN)
-        load_words(LOGSTD, 1)
-        load_words(MEAN, 1)
+        nc.scalar.dma_start(out=var_in[:], in_=s_var_view)
+        nc.scalar.dma_start(out=mu_in[:], in_=s_mu_view)
+        nc.scalar.dma_start(out=weight_in[:], in_=s_weight_view)
+        for w in (LOGSTD, MEAN):
+            nc.scalar.dma_start(out=bias_rows[0:1, w, :], in_=bias_in[w].unsqueeze(0))
+        for r in range(ROW_TILES):
+            nc.sync.dma_start(out=x_sb[:, r, :], in_=x_view[:, r, :])
+        for w in (LOGSTD, MEAN):
+            load_scales(w)
+            for h in range(HALVES):
+                load_words(w, h)
+
+        def over_components(small):
+            pairs = small.rearrange("p r (j g) -> p (r j) g", g=GAUSS)
+            return pairs.unsqueeze(2).to_broadcast([P, ROW_TILES * LABELS, COMPONENTS, GAUSS])
+
+        def as_jtg(table):
+            return table.rearrange("p r (j t g) -> p (r j) t g", t=COMPONENTS, g=GAUSS)
+
+        nc.scalar.activation(out=as_jtg(inv_e1_sb[:]), in_=over_components(var_in[:]), func=ACT.Exp, scale=-2.0)
+        nc.scalar.activation(
+            out=as_jtg(plus_one_sb[:, LOGSTD]), in_=over_components(var_in[:]), func=ACT.Identity, bias=one_col[:]
+        )
+        nc.scalar.activation(
+            out=as_jtg(plus_one_sb[:, MEAN]), in_=over_components(mu_in[:]), func=ACT.Identity, bias=one_col[:]
+        )
+        nc.scalar.copy(out=as_jtg(v1_sb[:]), in_=over_components(var_in[:]))
+        nc.scalar.activation(out=unused_col[:], in_=one_col[:], func=ACT.Sigmoid)
+
+        var_pairs = var_in[:].rearrange("p r (j g) -> p (r j) g", g=GAUSS)
+        nc.vector.tensor_tensor(out=v_sum[:], in0=var_pairs[:, :, 0], in1=var_pairs[:, :, 1], op=ALU.add)
+        both = [P, ROW_TILES * LABELS, COMPONENTS]
+        nc.vector.scalar_tensor_tensor(
+            out=c_sb[:].rearrange("p r (j t) -> p (r j) t", t=COMPONENTS),
+            in0=weight_in[:].rearrange("p r j -> p (r j)").unsqueeze(2).to_broadcast(both),
+            scalar=LOG_2PI,
+            in1=v_sum[:].unsqueeze(2).to_broadcast(both),
+            op0=ALU.subtract,
+            op1=ALU.subtract,
+        )
 
         x_words = x_sb[:].bitcast(F32)
 
@@ -180,201 +194,139 @@ def tile_chainlveg_pa_kernel(
             return grouped
 
         def quantise(r, grouped):
-            for g in range(PASSES):
-                nc.vector.quantize_mx(
-                    out=x_codes[:, g, rows(r)].bitcast(FP8X4),
-                    scales=x_planes[:, g, rows(r)],
-                    in_=grouped[:, g * K_PASS : (g + 1) * K_PASS],
-                )
+            nc.vector.quantize_mx(
+                out=x_codes[:, r, :].bitcast(FP8X4), scales=x_planes[:, r, :], in_=grouped[:]
+            )
 
         xt0 = transpose_rows(0)
         xt1 = transpose_rows(1)
         xt2 = transpose_rows(2)
         grouped0 = regroup(xt0)
-        nc.vector.tensor_copy(out=bias_rows_f32[:], in_=bias_rows[:])
-        bias_cols = bank_ps.tile([P, P], F32, name="bias_cols", tag="bank")
-        nc.tensor.transpose(bias_cols[:], bias_rows_f32[:], ident[:])
         grouped1 = regroup(xt1)
         quantise(0, grouped0)
         grouped2 = regroup(xt2)
         quantise(1, grouped1)
-        nc.vector.tensor_scalar(
-            out=one_minus_bias[:],
-            in0=bias_cols[:, 0 : 2 * BLOCKS],
-            scalar1=-1.0,
-            scalar2=1.0,
-            op0=ALU.mult,
-            op1=ALU.add,
-        )
         quantise(2, grouped2)
 
-        def over_components(small):
-            pairs = small.rearrange("p r (j g) -> p (r j) g", g=GAUSS)
-            return pairs.unsqueeze(2).to_broadcast([P, ROW_TILES * LABELS, COMPONENTS, GAUSS])
+        def table_to_psum(table_ps, table_sb):
+            nc.tensor.matmul(out=table_ps, lhsT=ident[:], rhs=table_sb, start=True, stop=True)
 
-        def as_jtg(table):
-            return table.rearrange("p r (j t g) -> p (r j) t g", t=COMPONENTS, g=GAUSS)
-
-        def twice(table):
-            return table.unsqueeze(2).to_broadcast([P, ROW_TILES, P // TABLE, TABLE])
-
-        def as_two(wide):
-            return wide.rearrange("p r (i c) -> p r i c", c=TABLE)
-
-        def transpose_table(table_ps, wide):
-            for r in range(ROW_TILES):
-                nc.tensor.transpose(table_ps[:, rows(r)], wide[:, r, :], ident[:])
-
-        nc.scalar.activation(out=r1_small[:], in_=var_in[:], func=ACT.Exp, scale=-2.0)
-        nc.scalar.activation(out=unused_col[:], in_=one_col[:], func=ACT.Sigmoid)
-
-        nc.vector.tensor_copy(out=as_jtg(v1_tab[:]), in_=over_components(var_in[:]))
-        nc.vector.tensor_scalar(
-            out=as_two(wide_v1[:]), in0=twice(v1_tab[:]), scalar1=-1.0, scalar2=1.0, op0=ALU.mult, op1=ALU.add
+        table_to_psum(
+            plus_one[:].rearrange("p w r c -> p (w r c)"), plus_one_sb[:].rearrange("p w r c -> p (w r c)")
         )
-        nc.vector.tensor_copy(out=as_jtg(m1_tab[:]), in_=over_components(mu_in[:]))
-        nc.vector.tensor_scalar(
-            out=as_two(wide_m1[:]), in0=twice(m1_tab[:]), scalar1=-1.0, scalar2=1.0, op0=ALU.mult, op1=ALU.add
-        )
-        nc.vector.tensor_copy(out=as_jtg(r1_tab[:]), in_=over_components(r1_small[:]))
-        nc.vector.tensor_copy(out=as_two(wide_r1[:]), in_=twice(r1_tab[:]))
-        ident_pairs = ident[:].rearrange("p (k g) -> p k g", g=GAUSS)
-        nc.vector.tensor_tensor(out=pair_pos[:], in0=ident_pairs[:, :, 0], in1=ident_pairs[:, :, 1], op=ALU.add)
-        nc.vector.tensor_scalar_mul(out=pair_neg[:], in0=pair_pos[:], scalar1=-1.0)
 
-        def project(w, b):
-            acc = bank_ps.tile([P, ROWS], F32, name="acc", tag="bank")
-            for moving in (slice(0, 2 * P), slice(2 * P, ROWS)):
-                for g in range(PASSES):
-                    nc.tensor.matmul_mx(
-                        out=acc[:, moving],
-                        lhsT=w_words[:, w, g, b * P : (b + 1) * P].bitcast(FP8X4),
-                        lhsT_scale=w_planes[w][4 * g : P, b * P : (b + 1) * P],
-                        rhs=x_codes[:, g, moving].bitcast(FP8X4),
-                        rhs_scale=x_planes[:, g, moving],
-                        start=(g == 0),
-                        stop=(g == PASSES - 1),
-                    )
-            nc.scalar.activation(
-                out=clipped[w][:, b, :],
-                in_=acc[:],
-                func=ACT.Relu,
-                bias=one_minus_bias[:, w * BLOCKS + b : w * BLOCKS + b + 1],
-                scale=-1.0,
-            )
+        for w in (LOGSTD, MEAN):
+            for h in range(HALVES):
+                spread = bank_ps.tile([P, BANK], F32, name="spread", tag="bank")
+                nc.tensor.matmul(out=spread[:], lhsT=ones[:], rhs=bias_rows[:, w, cols(h)], start=True, stop=True)
+                nc.scalar.copy(out=bias_all[:, w, cols(h)], in_=spread[:])
 
-        def project_group(w, h):
-            for b in range(h * GROUP, (h + 1) * GROUP):
-                project(w, b)
-
-        def for_each_block(table_ps):
-            return table_ps[:].unsqueeze(1).to_broadcast([P, GROUP, ROWS])
-
-        def lower_clip_minus(t, h, table_ps):
-            nc.vector.scalar_tensor_tensor(
-                out=t[:, blocks(h), :],
-                in0=t[:, blocks(h), :],
-                scalar=2.0,
-                in1=for_each_block(table_ps),
-                op0=ALU.min,
-                op1=ALU.subtract,
-            )
-
-        def share_of(h):
-            lower_clip_minus(share, h, one_minus_v1)
-            nc.scalar.activation(out=share[:, blocks(h), :], in_=share[:, blocks(h), :], func=ACT.Sigmoid, scale=2.0)
-
-        def gap_of(h):
-            lower_clip_minus(gap, h, one_minus_m1)
+        def project(w, h, r):
+            acc = bank_ps.tile([P, BANK], F32, name="acc", tag="bank")
+            for g in range(PASSES):
+                nc.tensor.matmul_mx(
+                    out=acc[:],
+                    lhsT=x_codes[:, r, g * P : (g + 1) * P].bitcast(FP8X4),
+                    lhsT_scale=x_planes[:, r, g * P : (g + 1) * P],
+                    rhs=w_words[:, w, g, cols(h)].bitcast(FP8X4),
+                    rhs_scale=w_planes[w][4 * g : P, cols(h)],
+                    start=(g == 0),
+                    stop=(g == PASSES - 1),
+                )
             nc.vector.tensor_tensor(
-                out=quad[:, blocks(h), :], in0=gap[:, blocks(h), :], in1=for_each_block(inv_e1), op=ALU.mult
+                out=proj[w][r][:, cols(h)], in0=acc[:], in1=bias_all[:, w, cols(h)], op=ALU.add
             )
 
-        def to_rows(src, h, r):
-            back = bank_ps.tile([P, GROUP, P], F32, name="back", tag="bank")
-            for k in range(GROUP):
-                nc.tensor.transpose(back[:, k, :], src[:, h * GROUP + k, rows(r)], ident[:])
-            return back
+        def lower_clip_plus_one(w, r):
+            t = proj[w][r]
+            nc.scalar.activation(out=t[:], in_=t[:], func=ACT.Relu, bias=one_col[:])
 
         def by_label(ap, width):
             return ap.rearrange("p (i c) -> p i c", c=width)
 
         def for_each_label(table, r, width):
-            return table[:, r, :].unsqueeze(1).to_broadcast([P, LABELS // GROUPS, width])
+            return table[:, r, :].unsqueeze(1).to_broadcast([P, LABELS, width])
 
-        def products_and_mu(h):
-            nc.vector.tensor_tensor(
-                out=gap_share[:, blocks(h), :], in0=gap[:, blocks(h), :], in1=share[:, blocks(h), :], op=ALU.mult
+        def upper_clip_minus_state(w, r):
+            t = proj[w][r]
+            nc.vector.scalar_tensor_tensor(
+                out=by_label(t[:], TABLE),
+                in0=by_label(t[:], TABLE),
+                scalar=2.0,
+                in1=for_each_label(plus_one[:, w], r, TABLE),
+                op0=ALU.min,
+                op1=ALU.subtract,
             )
+
+        for r in range(ROW_TILES):
+            project(LOGSTD, 0, r)
+        for r in range(ROW_TILES):
+            project(LOGSTD, 1, r)
+            lower_clip_plus_one(LOGSTD, r)
+
+        def project_mean(r):
+            for h in range(HALVES):
+                project(MEAN, h, r)
+            lower_clip_plus_one(MEAN, r)
+
+        project_mean(0)
+        table_to_psum(inv_e1.rearrange("p r c -> p (r c)"), inv_e1_sb[:].rearrange("p r c -> p (r c)"))
+        for r in range(ROW_TILES):
+            share, d = proj[LOGSTD][r], proj[MEAN][r]
+            upper_clip_minus_state(LOGSTD, r)
+            nc.scalar.activation(out=share[:], in_=share[:], func=ACT.Sigmoid, scale=-2.0)
+            if r + 1 < ROW_TILES:
+                project_mean(r + 1)
+            upper_clip_minus_state(MEAN, r)
+            nc.gpsimd.tensor_tensor(out=d_share[r][:], in0=d[:], in1=share[:], op=ALU.mult)
             nc.vector.tensor_tensor(
-                out=quad[:, blocks(h), :], in0=quad[:, blocks(h), :], in1=gap_share[:, blocks(h), :], op=ALU.mult
+                out=by_label(quad[r][:], TABLE),
+                in0=by_label(d[:], TABLE),
+                in1=for_each_label(inv_e1, r, TABLE),
+                op=ALU.mult,
             )
-            for r in range(ROW_TILES):
-                back = to_rows(gap_share, h, r)
-                nc.vector.tensor_tensor(
-                    out=by_label(mu_sb[:, r, columns(h, P)], TABLE),
-                    in0=for_each_label(m1_tab, r, TABLE),
-                    in1=back[:].rearrange("p k (i c) -> p (k i) c", c=TABLE),
-                    op=ALU.subtract,
-                )
-            nc.sync.dma_start(out=mu_out[:, :, columns(h, P)], in_=mu_sb[:, :, columns(h, P)])
+            nc.gpsimd.tensor_tensor(out=quad[r][:], in0=quad[r][:], in1=d_share[r][:], op=ALU.mult)
 
-        project_group(LOGSTD, 0)
-        transpose_table(one_minus_v1, wide_v1)
-        project_group(MEAN, 0)
-        transpose_table(one_minus_m1, wide_m1)
-        transpose_table(inv_e1, wide_r1)
-        share_of(0)
-        gap_of(0)
-        var_pairs = var_in[:].rearrange("p r (j g) -> p (r j) g", g=GAUSS)
-        nc.vector.tensor_tensor(out=v_sum[:], in0=var_pairs[:, :, 0], in1=var_pairs[:, :, 1], op=ALU.add)
-        both = [P, ROW_TILES * LABELS, COMPONENTS]
-        nc.vector.scalar_tensor_tensor(
-            out=c_tab[:].rearrange("p r (j t) -> p (r j) t", t=COMPONENTS),
-            in0=weight_in[:].rearrange("p r j -> p (r j)").unsqueeze(2).to_broadcast(both),
-            scalar=LOG_2PI,
-            in1=v_sum[:].unsqueeze(2).to_broadcast(both),
-            op0=ALU.subtract,
-            op1=ALU.subtract,
-        )
-        project_group(LOGSTD, 1)
-        project_group(MEAN, 1)
-        share_of(1)
-        products_and_mu(0)
-        gap_of(1)
-        products_and_mu(1)
+        table_to_psum(v1_tab.rearrange("p r c -> p (r c)"), v1_sb[:].rearrange("p r c -> p (r c)"))
+        table_to_psum(c_tab.rearrange("p r c -> p (r c)"), c_sb[:].rearrange("p r c -> p (r c)"))
 
-        for h in range(GROUPS):
-            nc.scalar.activation(out=log_share[:, blocks(h), :], in_=share[:, blocks(h), :], func=ACT.Ln)
+        for r in range(ROW_TILES):
             nc.scalar.activation(
-                out=log_rest[:, blocks(h), :], in_=share[:, blocks(h), :], func=ACT.Ln, bias=one_col[:], scale=-1.0
+                out=log_rest[r][:], in_=proj[LOGSTD][r][:], func=ACT.Ln, bias=one_col[:], scale=-1.0
             )
-        for h in range(GROUPS):
-            for r in range(ROW_TILES):
-                back = to_rows(log_rest, h, r)
-                nc.vector.scalar_tensor_tensor(
-                    out=by_label(var_sb[:, r, columns(h, P)], TABLE),
-                    in0=back[:].rearrange("p k (i c) -> p (k i) c", c=TABLE),
-                    scalar=0.5,
-                    in1=for_each_label(v1_tab, r, TABLE),
-                    op0=ALU.mult,
-                    op1=ALU.add,
-                )
-            nc.sync.dma_start(out=var_out[:, :, columns(h, P)], in_=var_sb[:, :, columns(h, P)])
-            for r in range(ROW_TILES):
-                sums = bank_ps.tile([P, GROUP, P // GAUSS], F32, name="sums", tag="bank")
-                for k in range(GROUP):
-                    b = h * GROUP + k
-                    nc.tensor.matmul(out=sums[:, k, :], lhsT=log_share[:, b, rows(r)], rhs=pair_neg[:], start=True, stop=False)
-                    nc.tensor.matmul(out=sums[:, k, :], lhsT=quad[:, b, rows(r)], rhs=pair_pos[:], start=False, stop=True)
-                nc.vector.scalar_tensor_tensor(
-                    out=by_label(scale_sb[:, r, columns(h, P // GAUSS)], LABELS * COMPONENTS),
-                    in0=sums[:].rearrange("p k (i c) -> p (k i) c", c=LABELS * COMPONENTS),
-                    scalar=-0.5,
-                    in1=for_each_label(c_tab, r, LABELS * COMPONENTS),
-                    op0=ALU.mult,
-                    op1=ALU.add,
-                )
-            nc.sync.dma_start(
-                out=scale_out[:, :, columns(h, P // GAUSS)], in_=scale_sb[:, :, columns(h, P // GAUSS)]
+        for r in range(ROW_TILES):
+            nc.scalar.activation(out=log_share[r][:], in_=proj[LOGSTD][r][:], func=ACT.Ln)
+        for r in range(ROW_TILES):
+            cs_mu = proj[MEAN][r]
+            nc.vector.scalar_tensor_tensor(
+                out=by_label(cs_mu[:], TABLE),
+                in0=by_label(d_share[r][:], TABLE),
+                scalar=1.0,
+                in1=for_each_label(plus_one[:, MEAN], r, TABLE),
+                op0=ALU.subtract,
+                op1=ALU.add,
             )
+            nc.sync.dma_start(out=mu_out[:, r, :], in_=cs_mu[:])
+        for r in range(ROW_TILES):
+            nc.vector.scalar_tensor_tensor(
+                out=by_label(log_rest[r][:], TABLE),
+                in0=by_label(log_rest[r][:], TABLE),
+                scalar=0.5,
+                in1=for_each_label(v1_tab, r, TABLE),
+                op0=ALU.mult,
+                op1=ALU.add,
+            )
+            nc.sync.dma_start(out=var_out[:, r, :], in_=log_rest[r][:])
+        for r in range(ROW_TILES):
+            nc.vector.tensor_tensor(out=quad[r][:], in0=quad[r][:], in1=log_share[r][:], op=ALU.subtract)
+            by_g = quad[r][:].rearrange("p (c g) -> p c g", g=GAUSS)
+            nc.vector.tensor_tensor(out=pair[r][:], in0=by_g[:, :, 0], in1=by_g[:, :, 1], op=ALU.add)
+            nc.vector.scalar_tensor_tensor(
+                out=by_label(pair[r][:], HALF_TABLE),
+                in0=by_label(pair[r][:], HALF_TABLE),
+                scalar=-0.5,
+                in1=for_each_label(c_tab, r, HALF_TABLE),
+                op0=ALU.mult,
+                op1=ALU.add,
+            )
+            nc.sync.dma_start(out=scale_out[:, r, :], in_=pair[r][:])

@@ -211,15 +211,13 @@ def tile_chainlveg_pa_kernel(
         def table_to_psum(table_ps, table_sb):
             nc.tensor.matmul(out=table_ps, lhsT=ident[:], rhs=table_sb, start=True, stop=True)
 
-        table_to_psum(
-            plus_one[:].rearrange("p w r c -> p (w r c)"), plus_one_sb[:].rearrange("p w r c -> p (w r c)")
-        )
-
-        for w in (LOGSTD, MEAN):
+        def spread_bias(w):
             for h in range(HALVES):
                 spread = bank_ps.tile([P, BANK], F32, name="spread", tag="bank")
                 nc.tensor.matmul(out=spread[:], lhsT=ones[:], rhs=bias_rows[:, w, cols(h)], start=True, stop=True)
                 nc.scalar.copy(out=bias_all[:, w, cols(h)], in_=spread[:])
+
+        spread_bias(LOGSTD)
 
         def project(w, h, r):
             acc = bank_ps.tile([P, BANK], F32, name="acc", tag="bank")
@@ -262,20 +260,37 @@ def tile_chainlveg_pa_kernel(
             project(LOGSTD, 0, r)
         for r in range(ROW_TILES):
             project(LOGSTD, 1, r)
-            lower_clip_plus_one(LOGSTD, r)
+        spread_bias(MEAN)
+        lower_clip_plus_one(LOGSTD, 0)
 
         def project_mean(r):
             for h in range(HALVES):
                 project(MEAN, h, r)
             lower_clip_plus_one(MEAN, r)
 
+        def finish_mu(r):
+            cs_mu = proj[MEAN][r]
+            nc.vector.scalar_tensor_tensor(
+                out=by_label(cs_mu[:], TABLE),
+                in0=by_label(d_share[r][:], TABLE),
+                scalar=1.0,
+                in1=for_each_label(plus_one[:, MEAN], r, TABLE),
+                op0=ALU.subtract,
+                op1=ALU.add,
+            )
+            nc.sync.dma_start(out=mu_out[:, r, :], in_=cs_mu[:])
+
         project_mean(0)
+        table_to_psum(
+            plus_one[:].rearrange("p w r c -> p (w r c)"), plus_one_sb[:].rearrange("p w r c -> p (w r c)")
+        )
         table_to_psum(inv_e1.rearrange("p r c -> p (r c)"), inv_e1_sb[:].rearrange("p r c -> p (r c)"))
         for r in range(ROW_TILES):
             share, d = proj[LOGSTD][r], proj[MEAN][r]
             upper_clip_minus_state(LOGSTD, r)
             nc.scalar.activation(out=share[:], in_=share[:], func=ACT.Sigmoid, scale=-2.0)
             if r + 1 < ROW_TILES:
+                lower_clip_plus_one(LOGSTD, r + 1)
                 project_mean(r + 1)
             upper_clip_minus_state(MEAN, r)
             nc.gpsimd.tensor_tensor(out=d_share[r][:], in0=d[:], in1=share[:], op=ALU.mult)
@@ -286,6 +301,8 @@ def tile_chainlveg_pa_kernel(
                 op=ALU.mult,
             )
             nc.gpsimd.tensor_tensor(out=quad[r][:], in0=quad[r][:], in1=d_share[r][:], op=ALU.mult)
+            if r > 0:
+                finish_mu(r - 1)
 
         table_to_psum(v1_tab.rearrange("p r c -> p (r c)"), v1_sb[:].rearrange("p r c -> p (r c)"))
         table_to_psum(c_tab.rearrange("p r c -> p (r c)"), c_sb[:].rearrange("p r c -> p (r c)"))
@@ -297,17 +314,6 @@ def tile_chainlveg_pa_kernel(
         for r in range(ROW_TILES):
             nc.scalar.activation(out=log_share[r][:], in_=proj[LOGSTD][r][:], func=ACT.Ln)
         for r in range(ROW_TILES):
-            cs_mu = proj[MEAN][r]
-            nc.vector.scalar_tensor_tensor(
-                out=by_label(cs_mu[:], TABLE),
-                in0=by_label(d_share[r][:], TABLE),
-                scalar=1.0,
-                in1=for_each_label(plus_one[:, MEAN], r, TABLE),
-                op0=ALU.subtract,
-                op1=ALU.add,
-            )
-            nc.sync.dma_start(out=mu_out[:, r, :], in_=cs_mu[:])
-        for r in range(ROW_TILES):
             nc.vector.scalar_tensor_tensor(
                 out=by_label(log_rest[r][:], TABLE),
                 in0=by_label(log_rest[r][:], TABLE),
@@ -317,6 +323,7 @@ def tile_chainlveg_pa_kernel(
                 op1=ALU.add,
             )
             nc.sync.dma_start(out=var_out[:, r, :], in_=log_rest[r][:])
+        finish_mu(ROW_TILES - 1)
         for r in range(ROW_TILES):
             nc.vector.tensor_tensor(out=quad[r][:], in0=quad[r][:], in1=log_share[r][:], op=ALU.subtract)
             by_g = quad[r][:].rearrange("p (c g) -> p c g", g=GAUSS)

@@ -23,14 +23,20 @@ LABELS = 16
 COMPONENTS = 2
 GAUSS = 2
 N = LABELS * LABELS * COMPONENTS * GAUSS
+COL_TILES = N // P
+GROUPS = 4
+PER_GROUP = COL_TILES // GROUPS
 BANK = 512
 HALVES = N // BANK
 STATE = LABELS * GAUSS
 TABLE = LABELS * COMPONENTS * GAUSS
 HALF_TABLE = LABELS * COMPONENTS
+PAIRS = P // GAUSS
 LOG_2PI = math.log(2.0 * math.pi)
 LOGSTD = 0
 MEAN = 1
+INV_E1 = 2
+ROW_SPLITS = ((0, 256), (256, 384))
 
 FLOPS = 2 * ROWS * K * 2 * N
 
@@ -70,54 +76,61 @@ def tile_chainlveg_pa_kernel(
     def cols(h):
         return slice(h * BANK, (h + 1) * BANK)
 
+    def rows(r):
+        return slice(r * P, (r + 1) * P)
+
+    def group(k):
+        return slice(k * PER_GROUP, (k + 1) * PER_GROUP)
+
     with ExitStack() as ctx:
         keep = ctx.enter_context(tc.tile_pool(name="keep", bufs=1))
-        stage = ctx.enter_context(tc.tile_pool(name="stage", bufs=ROW_TILES))
         tab_ps = ctx.enter_context(tc.psum_pool(name="tab_ps", bufs=1))
-        bank_ps = ctx.enter_context(tc.psum_pool(name="bank_ps", bufs=6))
+        bank_ps = ctx.enter_context(tc.psum_pool(name="bank_ps", bufs=5))
         ctx.enter_context(tc.manual_schedule())
 
         x_sb = keep.tile([P, ROW_TILES, K], BF16)
         ident = keep.tile([P, P], F32)
-        ones = keep.tile([P, P], BF16)
-        bias_rows = keep.tile([P, 2, N], BF16)
-        bias_all = keep.tile([P, 2, N], F32)
+        ident_bf = keep.tile([P, P], BF16)
+        bias_rows = keep.tile([P, P], BF16)
+        bias1 = keep.tile([P, 2 * COL_TILES], F32)
         one_col = keep.tile([P, 1], F32)
         unused_col = keep.tile([P, 1], F32)
         w_words = keep.tile([P, 2, PASSES, N], U32, align_bytes=64)
         w_planes = [keep.tile([P, N], U8, name="w_planes%d" % w, align_bytes=64) for w in range(2)]
-        x_codes = keep.tile([P, ROW_TILES, PASSES * P], U32, align_bytes=64)
-        x_planes = keep.tile([P, ROW_TILES, PASSES * P], U8, align_bytes=64)
-        mu_in = keep.tile([P, ROW_TILES, STATE], BF16)
-        var_in = keep.tile([P, ROW_TILES, STATE], BF16)
+        grouped = keep.tile([P, PASSES, 4 * ROWS], BF16, align_bytes=64)
+        x_codes = keep.tile([P, PASSES, ROWS], U32, align_bytes=64)
+        x_planes = keep.tile([P, PASSES, ROWS], U8, align_bytes=64)
+        state_in = keep.tile([P, 2, ROW_TILES, STATE], BF16)
         weight_in = keep.tile([P, ROW_TILES, LABELS], BF16)
         v_sum = keep.tile([P, ROW_TILES * LABELS], F32)
-        plus_one_sb = keep.tile([P, 2, ROW_TILES, TABLE], F32)
-        inv_e1_sb = keep.tile([P, ROW_TILES, TABLE], F32)
-        v1_sb = keep.tile([P, ROW_TILES, TABLE], F32)
-        c_sb = keep.tile([P, ROW_TILES, HALF_TABLE], F32)
-        plus_one = tab_ps.tile([P, 2, ROW_TILES, TABLE], F32)
-        others = tab_ps.tile([P, 2 * ROW_TILES * TABLE + ROW_TILES * HALF_TABLE], F32)
-        inv_e1 = others[:, 0 : ROW_TILES * TABLE].rearrange("p (r c) -> p r c", c=TABLE)
-        v1_tab = others[:, ROW_TILES * TABLE : 2 * ROW_TILES * TABLE].rearrange("p (r c) -> p r c", c=TABLE)
-        c_tab = others[:, 2 * ROW_TILES * TABLE :].rearrange("p (r c) -> p r c", c=HALF_TABLE)
+        w_shift = keep.tile([P, ROW_TILES * LABELS], F32)
+        tabs = keep.tile([P, 3, ROW_TILES, TABLE], F32)
+        rep = keep.tile([P, 3, ROW_TILES, 2 * TABLE], F32)
+        v1_tab = keep.tile([P, ROW_TILES, TABLE], F32)
+        c_tab = keep.tile([P, ROW_TILES, HALF_TABLE], F32)
+        pair_sum = keep.tile([P, PAIRS], F32)
+        pair_q = keep.tile([P, PAIRS], F32)
+        pair_l = keep.tile([P, PAIRS], F32)
 
-        def per_row_tile(label, width):
-            return [keep.tile([P, width], F32, name="%s%d" % (label, r)) for r in range(ROW_TILES)]
+        share = keep.tile([P, COL_TILES, ROWS], F32)
+        d = keep.tile([P, COL_TILES, ROWS], F32)
+        d_share = keep.tile([P, COL_TILES, ROWS], F32)
+        quad = keep.tile([P, COL_TILES, ROWS], F32)
+        log_share = keep.tile([P, COL_TILES, ROWS], F32)
+        log_rest = keep.tile([P, COL_TILES, ROWS], F32)
+        proj = [share, d]
+        mu_sb = keep.tile([P, ROW_TILES, N], F32)
+        var_sb = keep.tile([P, ROW_TILES, N], F32)
+        scale_sb = keep.tile([P, ROW_TILES, N // GAUSS], F32)
 
-        proj = [per_row_tile("logstd", N), per_row_tile("mean", N)]
-        d_share = per_row_tile("d_share", N)
-        quad = per_row_tile("quad", N)
-        log_share = per_row_tile("log_share", N)
-        log_rest = per_row_tile("log_rest", N)
-        pair = per_row_tile("pair", N // GAUSS)
+        turned = [tab_ps.tile([P, ROWS], F32, name="turned%d" % i, tag="tab%d" % i) for i in range(3)]
 
+        nc.vector.memset(one_col[:], 1.0)
+        nc.vector.memset(bias_rows[:], 0.0)
         for w in range(2):
             nc.vector.memset(w_planes[w][:].bitcast(I32), 0)
-        nc.vector.memset(bias_rows[:], 0.0)
-        nc.vector.memset(ones[:], 1.0)
-        nc.vector.memset(one_col[:], 1.0)
         make_identity(nc, ident[:])
+        make_identity(nc, ident_bf[:])
 
         def load_scales(w):
             for quadrant in range(4):
@@ -126,55 +139,77 @@ def tile_chainlveg_pa_kernel(
                     in_=scales_in[w][:, 4 * quadrant : 4 * quadrant + 4, :].bitcast(I32),
                 )
 
-        def load_words(w, h):
+        def load_words(w, lo, hi):
             by_partition = words_in[w].rearrange("g p n t -> p g (n t)")
             nc.sync.dma_start(
-                out=w_words[:, w, :, cols(h)].bitcast(I32),
-                in_=by_partition[:, :, 4 * h * BANK : 4 * (h + 1) * BANK].bitcast(I32),
+                out=w_words[:, w, :, lo:hi].bitcast(I32),
+                in_=by_partition[:, :, 4 * lo : 4 * hi].bitcast(I32),
             )
 
-        nc.scalar.dma_start(out=var_in[:], in_=s_var_view)
-        nc.scalar.dma_start(out=mu_in[:], in_=s_mu_view)
-        nc.scalar.dma_start(out=weight_in[:], in_=s_weight_view)
+        nc.scalar.dma_start(out=state_in[:, 0], in_=s_var_view)
+        nc.scalar.dma_start(out=state_in[:, 1], in_=s_mu_view)
         for w in (LOGSTD, MEAN):
-            nc.scalar.dma_start(out=bias_rows[0:1, w, :], in_=bias_in[w].unsqueeze(0))
+            nc.scalar.dma_start(
+                out=bias_rows[COL_TILES * w : COL_TILES * (w + 1), :],
+                in_=bias_in[w].rearrange("(a p) -> a p", p=P),
+            )
+        nc.scalar.dma_start(out=weight_in[:], in_=s_weight_view)
         for r in range(ROW_TILES):
             nc.sync.dma_start(out=x_sb[:, r, :], in_=x_view[:, r, :])
         for w in (LOGSTD, MEAN):
             load_scales(w)
-            for h in range(HALVES):
-                load_words(w, h)
+        for lo, hi in ((0, 256), (256, 512), (512, 1024)):
+            for w in (LOGSTD, MEAN):
+                load_words(w, lo, hi)
 
-        def over_components(small):
+        def over_components(small, n_outer):
             pairs = small.rearrange("p r (j g) -> p (r j) g", g=GAUSS)
-            return pairs.unsqueeze(2).to_broadcast([P, ROW_TILES * LABELS, COMPONENTS, GAUSS])
+            return pairs.unsqueeze(2).to_broadcast([P, n_outer * LABELS, COMPONENTS, GAUSS])
 
         def as_jtg(table):
             return table.rearrange("p r (j t g) -> p (r j) t g", t=COMPONENTS, g=GAUSS)
 
-        nc.scalar.activation(out=as_jtg(inv_e1_sb[:]), in_=over_components(var_in[:]), func=ACT.Exp, scale=-2.0)
+        var_in = state_in[:, 0]
         nc.scalar.activation(
-            out=as_jtg(plus_one_sb[:, LOGSTD]), in_=over_components(var_in[:]), func=ACT.Identity, bias=one_col[:]
+            out=as_jtg(tabs[:, INV_E1]), in_=over_components(var_in, ROW_TILES), func=ACT.Exp, scale=-2.0
         )
-        nc.scalar.activation(
-            out=as_jtg(plus_one_sb[:, MEAN]), in_=over_components(mu_in[:]), func=ACT.Identity, bias=one_col[:]
-        )
-        nc.scalar.copy(out=as_jtg(v1_sb[:]), in_=over_components(var_in[:]))
         nc.scalar.activation(out=unused_col[:], in_=one_col[:], func=ACT.Sigmoid)
-
-        var_pairs = var_in[:].rearrange("p r (j g) -> p (r j) g", g=GAUSS)
-        nc.vector.tensor_tensor(out=v_sum[:], in0=var_pairs[:, :, 0], in1=var_pairs[:, :, 1], op=ALU.add)
-        both = [P, ROW_TILES * LABELS, COMPONENTS]
-        nc.vector.scalar_tensor_tensor(
-            out=c_sb[:].rearrange("p r (j t) -> p (r j) t", t=COMPONENTS),
-            in0=weight_in[:].rearrange("p r j -> p (r j)").unsqueeze(2).to_broadcast(both),
-            scalar=LOG_2PI,
-            in1=v_sum[:].unsqueeze(2).to_broadcast(both),
-            op0=ALU.subtract,
-            op1=ALU.subtract,
+        nc.vector.tensor_scalar(
+            out=as_jtg(tabs[:, 0:2].rearrange("p w r c -> p (w r) c")),
+            in0=over_components(state_in[:].rearrange("p w r c -> p (w r) c"), 2 * ROW_TILES),
+            scalar1=1.0,
+            scalar2=None,
+            op0=ALU.add,
         )
+        nc.vector.tensor_copy(
+            out=rep[:].rearrange("p w r (i c) -> p (w r) i c", i=2),
+            in_=tabs[:].rearrange("p w r c -> p (w r) c").unsqueeze(2).to_broadcast([P, 3 * ROW_TILES, 2, TABLE]),
+        )
+
+        nc.gpsimd.tensor_copy(out=as_jtg(v1_tab[:]), in_=over_components(var_in, ROW_TILES))
+        var_pairs = var_in.rearrange("p r (j g) -> p (r j) g", g=GAUSS)
+        nc.gpsimd.tensor_tensor(out=v_sum[:], in0=var_pairs[:, :, 0], in1=var_pairs[:, :, 1], op=ALU.add)
+        nc.gpsimd.tensor_scalar(
+            out=w_shift[:],
+            in0=weight_in[:].rearrange("p r j -> p (r j)"),
+            scalar1=LOG_2PI,
+            scalar2=None,
+            op0=ALU.subtract,
+        )
+        both = [P, ROW_TILES * LABELS, COMPONENTS]
+        nc.gpsimd.tensor_tensor(
+            out=c_tab[:].rearrange("p r (j t) -> p (r j) t", t=COMPONENTS),
+            in0=w_shift[:].unsqueeze(2).to_broadcast(both),
+            in1=v_sum[:].unsqueeze(2).to_broadcast(both),
+            op=ALU.subtract,
+        )
+        by_pair = ident[:].rearrange("p (c g) -> p c g", g=GAUSS)
+        nc.gpsimd.tensor_tensor(out=pair_sum[:], in0=by_pair[:, :, 0], in1=by_pair[:, :, 1], op=ALU.add)
+        nc.gpsimd.tensor_scalar(out=pair_q[:], in0=pair_sum[:], scalar1=-0.5, scalar2=None, op0=ALU.mult)
+        nc.gpsimd.tensor_scalar(out=pair_l[:], in0=pair_sum[:], scalar1=0.5, scalar2=None, op0=ALU.mult)
 
         x_words = x_sb[:].bitcast(F32)
+        grouped_words = grouped[:].bitcast(F32)
 
         def transpose_rows(r):
             xt = bank_ps.tile([P, 2 * PASSES, P], F32, name="xt", tag="bank")
@@ -185,155 +220,198 @@ def tile_chainlveg_pa_kernel(
                     )
             return xt
 
-        def regroup(xt):
-            grouped = stage.tile([P, K], BF16, name="grouped", tag="grouped", align_bytes=64)
+        def regroup(r, xt):
             nc.vector.tensor_copy(
-                out=grouped[:].bitcast(F32).rearrange("p (g m u) -> p g m u", g=PASSES, u=2),
+                out=grouped_words[:, :, 2 * P * r : 2 * P * (r + 1)].rearrange("p g (m u) -> p g m u", u=2),
                 in_=xt[:].rearrange("p (g u) m -> p g m u", u=2),
             )
-            return grouped
 
-        def quantise(r, grouped):
+        def quantise(g, lo, hi):
             nc.vector.quantize_mx(
-                out=x_codes[:, r, :].bitcast(FP8X4), scales=x_planes[:, r, :], in_=grouped[:]
+                out=x_codes[:, g, lo:hi].bitcast(FP8X4),
+                scales=x_planes[:, g, lo:hi],
+                in_=grouped[:, g, 4 * lo : 4 * hi],
             )
 
-        xt0 = transpose_rows(0)
-        xt1 = transpose_rows(1)
-        xt2 = transpose_rows(2)
-        grouped0 = regroup(xt0)
-        grouped1 = regroup(xt1)
-        quantise(0, grouped0)
-        grouped2 = regroup(xt2)
-        quantise(1, grouped1)
-        quantise(2, grouped2)
+        xts = [transpose_rows(r) for r in range(ROW_TILES)]
+        bias_t = bank_ps.tile([P, P], BF16, name="bias_t", tag="bank")
+        nc.tensor.transpose(bias_t[:], bias_rows[:], ident_bf[:])
+        nc.scalar.activation(out=bias1[:], in_=bias_t[:, 0 : 2 * COL_TILES], func=ACT.Identity, bias=one_col[:])
+        regroup(0, xts[0])
+        regroup(1, xts[1])
+        for i in range(3):
+            for r in range(ROW_TILES):
+                nc.tensor.transpose(turned[i][:, rows(r)], rep[:, i, r, :], ident[:])
+        quantise(0, 0, 256)
+        regroup(2, xts[2])
+        quantise(1, 0, 256)
+        quantise(0, 256, 384)
+        quantise(1, 256, 384)
 
-        def table_to_psum(table_ps, table_sb):
-            nc.tensor.matmul(out=table_ps, lhsT=ident[:], rhs=table_sb, start=True, stop=True)
-
-        def spread_bias(w):
-            for h in range(HALVES):
-                spread = bank_ps.tile([P, BANK], F32, name="spread", tag="bank")
-                nc.tensor.matmul(out=spread[:], lhsT=ones[:], rhs=bias_rows[:, w, cols(h)], start=True, stop=True)
-                nc.scalar.copy(out=bias_all[:, w, cols(h)], in_=spread[:])
-
-        spread_bias(LOGSTD)
-
-        def project(w, h, r):
-            acc = bank_ps.tile([P, BANK], F32, name="acc", tag="bank")
-            for g in range(PASSES):
-                nc.tensor.matmul_mx(
-                    out=acc[:],
-                    lhsT=x_codes[:, r, g * P : (g + 1) * P].bitcast(FP8X4),
-                    lhsT_scale=x_planes[:, r, g * P : (g + 1) * P],
-                    rhs=w_words[:, w, g, cols(h)].bitcast(FP8X4),
-                    rhs_scale=w_planes[w][4 * g : P, cols(h)],
-                    start=(g == 0),
-                    stop=(g == PASSES - 1),
+        def project(w, k):
+            for a in range(k * PER_GROUP, (k + 1) * PER_GROUP):
+                acc = bank_ps.tile([P, ROWS], F32, name="acc", tag="bank")
+                for lo, hi in ROW_SPLITS:
+                    for g in range(PASSES):
+                        nc.tensor.matmul_mx(
+                            out=acc[:, lo:hi],
+                            lhsT=w_words[:, w, g, a * P : (a + 1) * P].bitcast(FP8X4),
+                            lhsT_scale=w_planes[w][4 * g : P, a * P : (a + 1) * P],
+                            rhs=x_codes[:, g, lo:hi].bitcast(FP8X4),
+                            rhs_scale=x_planes[:, g, lo:hi],
+                            start=(g == 0),
+                            stop=(g == PASSES - 1),
+                        )
+                nc.scalar.activation(
+                    out=proj[w][:, a, :],
+                    in_=acc[:],
+                    func=ACT.Relu,
+                    bias=bias1[:, COL_TILES * w + a : COL_TILES * w + a + 1],
                 )
-            nc.vector.tensor_tensor(
-                out=proj[w][r][:, cols(h)], in0=acc[:], in1=bias_all[:, w, cols(h)], op=ALU.add
+
+        def for_each_tile(table):
+            return table[:].unsqueeze(1).to_broadcast([P, PER_GROUP, ROWS])
+
+        def minus_state(w, k):
+            t = proj[w][:, group(k), :]
+            nc.vector.scalar_tensor_tensor(
+                out=t, in0=t, scalar=2.0, in1=for_each_tile(turned[w]), op0=ALU.min, op1=ALU.subtract
             )
 
-        def lower_clip_plus_one(w, r):
-            t = proj[w][r]
-            nc.scalar.activation(out=t[:], in_=t[:], func=ACT.Relu, bias=one_col[:])
+        def sigmoid(k):
+            nc.scalar.activation(out=share[:, group(k), :], in_=share[:, group(k), :], func=ACT.Sigmoid, scale=-2.0)
+
+        def d_over_e1(k):
+            nc.vector.tensor_tensor(
+                out=quad[:, group(k), :], in0=d[:, group(k), :], in1=for_each_tile(turned[INV_E1]), op=ALU.mult
+            )
+
+        def d_times_share(k):
+            nc.gpsimd.tensor_tensor(
+                out=d_share[:, group(k), :], in0=d[:, group(k), :], in1=share[:, group(k), :], op=ALU.mult
+            )
+
+        def finish_quad(k):
+            nc.gpsimd.tensor_tensor(
+                out=quad[:, group(k), :], in0=quad[:, group(k), :], in1=d_share[:, group(k), :], op=ALU.mult
+            )
+
+        def new_banks():
+            return [bank_ps.tile([P, BANK], F32, name="back", tag="bank") for r in range(ROW_TILES)]
+
+        def turn_back(src, k, banks):
+            for r in range(ROW_TILES):
+                for a in range(k * PER_GROUP, (k + 1) * PER_GROUP):
+                    slot = a % (COL_TILES // HALVES)
+                    nc.tensor.transpose(banks[r][:, slot * P : (slot + 1) * P], src[:, a, rows(r)], ident[:])
 
         def by_label(ap, width):
             return ap.rearrange("p (i c) -> p i c", c=width)
 
-        def for_each_label(table, r, width):
-            return table[:, r, :].unsqueeze(1).to_broadcast([P, LABELS, width])
+        def for_each_label(table, r, width, n_labels):
+            return table[:, r, :].unsqueeze(1).to_broadcast([P, n_labels, width])
 
-        def upper_clip_minus_state(w, r):
-            t = proj[w][r]
-            nc.vector.scalar_tensor_tensor(
-                out=by_label(t[:], TABLE),
-                in0=by_label(t[:], TABLE),
-                scalar=2.0,
-                in1=for_each_label(plus_one[:, w], r, TABLE),
-                op0=ALU.min,
-                op1=ALU.subtract,
+        def finish_mu(h, banks):
+            for r in range(ROW_TILES):
+                nc.vector.scalar_tensor_tensor(
+                    out=by_label(mu_sb[:, r, cols(h)], TABLE),
+                    in0=by_label(banks[r][:], TABLE),
+                    scalar=1.0,
+                    in1=for_each_label(tabs[:, MEAN], r, TABLE, BANK // TABLE),
+                    op0=ALU.subtract,
+                    op1=ALU.add,
+                )
+                nc.sync.dma_start(out=mu_out[:, r, cols(h)], in_=mu_sb[:, r, cols(h)])
+
+        def finish_var(h, banks):
+            for r in range(ROW_TILES):
+                nc.vector.scalar_tensor_tensor(
+                    out=by_label(var_sb[:, r, cols(h)], TABLE),
+                    in0=by_label(banks[r][:], TABLE),
+                    scalar=0.5,
+                    in1=for_each_label(v1_tab, r, TABLE, BANK // TABLE),
+                    op0=ALU.mult,
+                    op1=ALU.add,
+                )
+                nc.sync.dma_start(out=var_out[:, r, cols(h)], in_=var_sb[:, r, cols(h)])
+
+        sums = []
+
+        def open_sum(r):
+            bank = tab_ps.tile([P, BANK], F32, name="sum%d" % r, tag="tab%d" % r)
+            nc.tensor.matmul(
+                out=by_label(bank[:], HALF_TABLE),
+                lhsT=ident[:],
+                rhs=for_each_label(c_tab, r, HALF_TABLE, LABELS),
+                start=True,
+                stop=False,
             )
+            sums.append(bank)
 
-        for r in range(ROW_TILES):
-            project(LOGSTD, 0, r)
-        for r in range(ROW_TILES):
-            project(LOGSTD, 1, r)
-        spread_bias(MEAN)
-        lower_clip_plus_one(LOGSTD, 0)
+        def add_pairs(src, k, pair, last):
+            for a in range(k * PER_GROUP, (k + 1) * PER_GROUP):
+                for r in range(ROW_TILES):
+                    nc.tensor.matmul(
+                        out=sums[r][:, a * PAIRS : (a + 1) * PAIRS],
+                        lhsT=src[:, a, rows(r)],
+                        rhs=pair[:],
+                        start=False,
+                        stop=(last and a == COL_TILES - 1),
+                    )
 
-        def project_mean(r):
-            for h in range(HALVES):
-                project(MEAN, h, r)
-            lower_clip_plus_one(MEAN, r)
-
-        def finish_mu(r):
-            cs_mu = proj[MEAN][r]
-            nc.vector.scalar_tensor_tensor(
-                out=by_label(cs_mu[:], TABLE),
-                in0=by_label(d_share[r][:], TABLE),
-                scalar=1.0,
-                in1=for_each_label(plus_one[:, MEAN], r, TABLE),
-                op0=ALU.subtract,
-                op1=ALU.add,
-            )
-            nc.sync.dma_start(out=mu_out[:, r, :], in_=cs_mu[:])
-
-        project_mean(0)
-        table_to_psum(
-            plus_one[:].rearrange("p w r c -> p (w r c)"), plus_one_sb[:].rearrange("p w r c -> p (w r c)")
-        )
-        table_to_psum(inv_e1.rearrange("p r c -> p (r c)"), inv_e1_sb[:].rearrange("p r c -> p (r c)"))
-        for r in range(ROW_TILES):
-            share, d = proj[LOGSTD][r], proj[MEAN][r]
-            upper_clip_minus_state(LOGSTD, r)
-            nc.scalar.activation(out=share[:], in_=share[:], func=ACT.Sigmoid, scale=-2.0)
-            if r + 1 < ROW_TILES:
-                lower_clip_plus_one(LOGSTD, r + 1)
-                project_mean(r + 1)
-            upper_clip_minus_state(MEAN, r)
-            nc.gpsimd.tensor_tensor(out=d_share[r][:], in0=d[:], in1=share[:], op=ALU.mult)
-            nc.vector.tensor_tensor(
-                out=by_label(quad[r][:], TABLE),
-                in0=by_label(d[:], TABLE),
-                in1=for_each_label(inv_e1, r, TABLE),
-                op=ALU.mult,
-            )
-            nc.gpsimd.tensor_tensor(out=quad[r][:], in0=quad[r][:], in1=d_share[r][:], op=ALU.mult)
-            if r > 0:
-                finish_mu(r - 1)
-
-        table_to_psum(v1_tab.rearrange("p r c -> p (r c)"), v1_sb[:].rearrange("p r c -> p (r c)"))
-        table_to_psum(c_tab.rearrange("p r c -> p (r c)"), c_sb[:].rearrange("p r c -> p (r c)"))
-
-        for r in range(ROW_TILES):
+        def log_of_rest(k):
             nc.scalar.activation(
-                out=log_rest[r][:], in_=proj[LOGSTD][r][:], func=ACT.Ln, bias=one_col[:], scale=-1.0
+                out=log_rest[:, group(k), :], in_=share[:, group(k), :], func=ACT.Ln, bias=one_col[:], scale=-1.0
             )
+
+        def log_of_share(k):
+            nc.scalar.activation(out=log_share[:, group(k), :], in_=share[:, group(k), :], func=ACT.Ln)
+
+        mu_banks = [None, None]
+        for k in range(GROUPS):
+            project(LOGSTD, k)
+            if k > 0:
+                sigmoid(k - 1)
+            minus_state(LOGSTD, k)
+            if k > 0:
+                d_over_e1(k - 1)
+                d_times_share(k - 1)
+            if k == 1:
+                finish_quad(0)
+            project(MEAN, k)
+            if k == 2:
+                mu_banks[0] = new_banks()
+                turn_back(d_share, 0, mu_banks[0])
+            minus_state(MEAN, k)
+        sigmoid(GROUPS - 1)
+        d_over_e1(GROUPS - 1)
+        d_times_share(GROUPS - 1)
+        for k in range(1, GROUPS):
+            finish_quad(k)
+
+        open_sum(0)
+        turn_back(d_share, 1, mu_banks[0])
+        finish_mu(0, mu_banks[0])
+        open_sum(1)
+        mu_banks[1] = new_banks()
+        turn_back(d_share, 2, mu_banks[1])
+        open_sum(2)
+        add_pairs(quad, 0, pair_q, False)
+        turn_back(d_share, 3, mu_banks[1])
+        finish_mu(1, mu_banks[1])
+        for h in range(HALVES):
+            var_banks = new_banks()
+            for k in (2 * h, 2 * h + 1):
+                log_of_rest(k)
+                turn_back(log_rest, k, var_banks)
+            finish_var(h, var_banks)
+        add_pairs(quad, 1, pair_q, False)
+        for k in range(GROUPS):
+            log_of_share(k)
+            add_pairs(log_share, k, pair_l, False)
+            if k == 1:
+                add_pairs(quad, 2, pair_q, False)
+        add_pairs(quad, 3, pair_q, True)
         for r in range(ROW_TILES):
-            nc.scalar.activation(out=log_share[r][:], in_=proj[LOGSTD][r][:], func=ACT.Ln)
-        for r in range(ROW_TILES):
-            nc.vector.scalar_tensor_tensor(
-                out=by_label(log_rest[r][:], TABLE),
-                in0=by_label(log_rest[r][:], TABLE),
-                scalar=0.5,
-                in1=for_each_label(v1_tab, r, TABLE),
-                op0=ALU.mult,
-                op1=ALU.add,
-            )
-            nc.sync.dma_start(out=var_out[:, r, :], in_=log_rest[r][:])
-        finish_mu(ROW_TILES - 1)
-        for r in range(ROW_TILES):
-            nc.vector.tensor_tensor(out=quad[r][:], in0=quad[r][:], in1=log_share[r][:], op=ALU.subtract)
-            by_g = quad[r][:].rearrange("p (c g) -> p c g", g=GAUSS)
-            nc.vector.tensor_tensor(out=pair[r][:], in0=by_g[:, :, 0], in1=by_g[:, :, 1], op=ALU.add)
-            nc.vector.scalar_tensor_tensor(
-                out=by_label(pair[r][:], HALF_TABLE),
-                in0=by_label(pair[r][:], HALF_TABLE),
-                scalar=-0.5,
-                in1=for_each_label(c_tab, r, HALF_TABLE),
-                op0=ALU.mult,
-                op1=ALU.add,
-            )
-            nc.sync.dma_start(out=scale_out[:, r, :], in_=pair[r][:])
+            nc.scalar.copy(out=scale_sb[:, r, :], in_=sums[r][:])
+            nc.sync.dma_start(out=scale_out[:, r, :], in_=scale_sb[:, r, :])

@@ -84,8 +84,7 @@ def tile_chainlveg_pa_kernel(
 
     with ExitStack() as ctx:
         keep = ctx.enter_context(tc.tile_pool(name="keep", bufs=1))
-        tab_ps = ctx.enter_context(tc.psum_pool(name="tab_ps", bufs=1))
-        bank_ps = ctx.enter_context(tc.psum_pool(name="bank_ps", bufs=5))
+        bank_ps = ctx.enter_context(tc.psum_pool(name="bank_ps", bufs=8))
         ctx.enter_context(tc.manual_schedule())
 
         x_sb = keep.tile([P, ROW_TILES, K], BF16)
@@ -108,9 +107,9 @@ def tile_chainlveg_pa_kernel(
         rep = keep.tile([P, 3, ROW_TILES, 2 * TABLE], F32)
         v1_tab = keep.tile([P, ROW_TILES, TABLE], F32)
         c_tab = keep.tile([P, ROW_TILES, HALF_TABLE], F32)
-        pair_sum = keep.tile([P, PAIRS], F32)
-        pair_q = keep.tile([P, PAIRS], F32)
-        pair_l = keep.tile([P, PAIRS], F32)
+        c_twice = keep.tile([P, ROW_TILES, 2 * HALF_TABLE], F32)
+        perm = keep.tile([P, P], F32)
+        half_sum = keep.tile([P, ROW_TILES, N // GAUSS], F32)
 
         share = keep.tile([P, COL_TILES, ROWS], F32)
         d = keep.tile([P, COL_TILES, ROWS], F32)
@@ -123,7 +122,7 @@ def tile_chainlveg_pa_kernel(
         var_sb = keep.tile([P, ROW_TILES, N], F32)
         scale_sb = keep.tile([P, ROW_TILES, N // GAUSS], F32)
 
-        turned = [tab_ps.tile([P, ROWS], F32, name="turned%d" % i, tag="tab%d" % i) for i in range(3)]
+        turned = [bank_ps.tile([P, ROWS], F32, name="turned%d" % i, tag="bank") for i in range(3)]
 
         nc.vector.memset(one_col[:], 1.0)
         nc.vector.memset(bias_rows[:], 0.0)
@@ -203,10 +202,13 @@ def tile_chainlveg_pa_kernel(
             in1=v_sum[:].unsqueeze(2).to_broadcast(both),
             op=ALU.subtract,
         )
-        by_pair = ident[:].rearrange("p (c g) -> p c g", g=GAUSS)
-        nc.gpsimd.tensor_tensor(out=pair_sum[:], in0=by_pair[:, :, 0], in1=by_pair[:, :, 1], op=ALU.add)
-        nc.gpsimd.tensor_scalar(out=pair_q[:], in0=pair_sum[:], scalar1=-0.5, scalar2=None, op0=ALU.mult)
-        nc.gpsimd.tensor_scalar(out=pair_l[:], in0=pair_sum[:], scalar1=0.5, scalar2=None, op0=ALU.mult)
+        nc.gpsimd.tensor_copy(
+            out=c_twice[:].rearrange("p r (i c) -> p r i c", i=2),
+            in_=c_tab[:].unsqueeze(2).to_broadcast([P, ROW_TILES, 2, HALF_TABLE]),
+        )
+        nc.gpsimd.tensor_copy(
+            out=perm[:].rearrange("p (g c) -> p g c", g=GAUSS), in_=ident[:].rearrange("p (c g) -> p g c", g=GAUSS)
+        )
 
         x_words = x_sb[:].bitcast(F32)
         grouped_words = grouped[:].bitcast(F32)
@@ -282,8 +284,13 @@ def tile_chainlveg_pa_kernel(
             nc.scalar.activation(out=share[:, group(k), :], in_=share[:, group(k), :], func=ACT.Sigmoid, scale=-2.0)
 
         def d_over_e1(k):
-            nc.vector.tensor_tensor(
-                out=quad[:, group(k), :], in0=d[:, group(k), :], in1=for_each_tile(turned[INV_E1]), op=ALU.mult
+            nc.vector.scalar_tensor_tensor(
+                out=quad[:, group(k), :],
+                in0=d[:, group(k), :],
+                scalar=-1.0,
+                in1=for_each_tile(turned[INV_E1]),
+                op0=ALU.mult,
+                op1=ALU.mult,
             )
 
         def d_times_share(k):
@@ -335,29 +342,41 @@ def tile_chainlveg_pa_kernel(
                 )
                 nc.sync.dma_start(out=var_out[:, r, cols(h)], in_=var_sb[:, r, cols(h)])
 
-        sums = []
+        def turn_pairs(k, banks):
+            for r in range(ROW_TILES):
+                for a in range(k * PER_GROUP, (k + 1) * PER_GROUP):
+                    slot = a % (COL_TILES // HALVES)
+                    for src, first in ((quad, True), (log_share, False)):
+                        nc.tensor.matmul(
+                            out=banks[r][:, slot * P : (slot + 1) * P],
+                            lhsT=src[:, a, rows(r)],
+                            rhs=perm[:],
+                            start=first,
+                            stop=not first,
+                            is_transpose=True,
+                        )
 
-        def open_sum(r):
-            bank = tab_ps.tile([P, BANK], F32, name="sum%d" % r, tag="tab%d" % r)
-            nc.tensor.matmul(
-                out=by_label(bank[:], HALF_TABLE),
-                lhsT=ident[:],
-                rhs=for_each_label(c_tab, r, HALF_TABLE, LABELS),
-                start=True,
-                stop=False,
-            )
-            sums.append(bank)
-
-        def add_pairs(src, k, pair, last):
-            for a in range(k * PER_GROUP, (k + 1) * PER_GROUP):
-                for r in range(ROW_TILES):
-                    nc.tensor.matmul(
-                        out=sums[r][:, a * PAIRS : (a + 1) * PAIRS],
-                        lhsT=src[:, a, rows(r)],
-                        rhs=pair[:],
-                        start=False,
-                        stop=(last and a == COL_TILES - 1),
-                    )
+        def finish_scale(h, banks):
+            half = slice(h * BANK // GAUSS, (h + 1) * BANK // GAUSS)
+            for r in range(ROW_TILES):
+                by_g = banks[r][:].rearrange("p (s g c) -> p s g c", g=GAUSS, c=PAIRS)
+                nc.vector.scalar_tensor_tensor(
+                    out=by_label(half_sum[:, r, half], PAIRS),
+                    in0=by_g[:, :, 0, :],
+                    scalar=0.5,
+                    in1=for_each_label(c_twice, r, PAIRS, COL_TILES // HALVES),
+                    op0=ALU.mult,
+                    op1=ALU.add,
+                )
+                nc.vector.scalar_tensor_tensor(
+                    out=by_label(scale_sb[:, r, half], PAIRS),
+                    in0=by_g[:, :, 1, :],
+                    scalar=0.5,
+                    in1=by_label(half_sum[:, r, half], PAIRS),
+                    op0=ALU.mult,
+                    op1=ALU.add,
+                )
+                nc.sync.dma_start(out=scale_out[:, r, half], in_=scale_sb[:, r, half])
 
         def log_of_rest(k):
             nc.scalar.activation(
@@ -389,14 +408,10 @@ def tile_chainlveg_pa_kernel(
         for k in range(1, GROUPS):
             finish_quad(k)
 
-        open_sum(0)
         turn_back(d_share, 1, mu_banks[0])
         finish_mu(0, mu_banks[0])
-        open_sum(1)
         mu_banks[1] = new_banks()
         turn_back(d_share, 2, mu_banks[1])
-        open_sum(2)
-        add_pairs(quad, 0, pair_q, False)
         turn_back(d_share, 3, mu_banks[1])
         finish_mu(1, mu_banks[1])
         for h in range(HALVES):
@@ -405,13 +420,8 @@ def tile_chainlveg_pa_kernel(
                 log_of_rest(k)
                 turn_back(log_rest, k, var_banks)
             finish_var(h, var_banks)
-        add_pairs(quad, 1, pair_q, False)
-        for k in range(GROUPS):
-            log_of_share(k)
-            add_pairs(log_share, k, pair_l, False)
-            if k == 1:
-                add_pairs(quad, 2, pair_q, False)
-        add_pairs(quad, 3, pair_q, True)
-        for r in range(ROW_TILES):
-            nc.scalar.copy(out=scale_sb[:, r, :], in_=sums[r][:])
-            nc.sync.dma_start(out=scale_out[:, r, :], in_=scale_sb[:, r, :])
+            pair_banks = new_banks()
+            for k in (2 * h, 2 * h + 1):
+                log_of_share(k)
+                turn_pairs(k, pair_banks)
+            finish_scale(h, pair_banks)

@@ -63,7 +63,7 @@ def tile_chainlveg_pa_kernel(
     bias_in = [tcv_b, tcm_b]
 
     def by_row_tile(flat):
-        return flat.rearrange("(r p) c -> p r c", p=P)
+        return flat.rearrange("(p r) c -> p r c", r=ROW_TILES)
 
     x_view = by_row_tile(x.flatten_outer_dims())
     s_mu_view = by_row_tile(s_mu.rearrange("b q j e g -> (b q) (j e g)"))
@@ -101,6 +101,9 @@ def tile_chainlveg_pa_kernel(
         x_planes = keep.tile([P, PASSES, ROWS], U8, align_bytes=64)
         state_in = keep.tile([P, 2, ROW_TILES, STATE], BF16)
         weight_in = keep.tile([P, ROW_TILES, LABELS], BF16)
+        sig_minus = keep.tile([P, ROW_TILES, STATE], F32)
+        sig_plus = keep.tile([P, ROW_TILES, STATE], F32)
+        inv_plus = keep.tile([P, ROW_TILES, STATE], F32)
         v_sum = keep.tile([P, ROW_TILES * LABELS], F32)
         w_shift = keep.tile([P, ROW_TILES * LABELS], F32)
         tabs = keep.tile([P, 3, ROW_TILES, TABLE], F32)
@@ -124,10 +127,10 @@ def tile_chainlveg_pa_kernel(
 
         turned = [bank_ps.tile([P, ROWS], F32, name="turned%d" % i, tag="bank") for i in range(3)]
 
-        nc.vector.memset(one_col[:], 1.0)
         nc.vector.memset(bias_rows[:], 0.0)
+        nc.vector.memset(one_col[:], 1.0)
         for w in range(2):
-            nc.vector.memset(w_planes[w][:].bitcast(I32), 0)
+            nc.gpsimd.memset(w_planes[w][:].bitcast(F32), 0.0)
         make_identity(nc, ident[:])
         make_identity(nc, ident_bf[:])
 
@@ -145,19 +148,19 @@ def tile_chainlveg_pa_kernel(
                 in_=by_partition[:, :, 4 * lo : 4 * hi].bitcast(I32),
             )
 
-        nc.scalar.dma_start(out=state_in[:, 0], in_=s_var_view)
-        nc.scalar.dma_start(out=state_in[:, 1], in_=s_mu_view)
+        for r in range(ROW_TILES):
+            nc.scalar.dma_start(out=x_sb[:, r, :], in_=x_view[:, r, :])
         for w in (LOGSTD, MEAN):
             nc.scalar.dma_start(
                 out=bias_rows[COL_TILES * w : COL_TILES * (w + 1), :],
                 in_=bias_in[w].rearrange("(a p) -> a p", p=P),
             )
-        nc.scalar.dma_start(out=weight_in[:], in_=s_weight_view)
-        for r in range(ROW_TILES):
-            nc.sync.dma_start(out=x_sb[:, r, :], in_=x_view[:, r, :])
+        nc.scalar.dma_start(out=state_in[:, 0], in_=s_var_view)
+        nc.scalar.dma_start(out=state_in[:, 1], in_=s_mu_view)
         for w in (LOGSTD, MEAN):
             load_scales(w)
-        for lo, hi in ((0, 256), (256, 512), (512, 1024)):
+            load_words(w, 0, 256)
+        for lo, hi in ((256, 512), (512, 1024)):
             for w in (LOGSTD, MEAN):
                 load_words(w, lo, hi)
 
@@ -169,21 +172,31 @@ def tile_chainlveg_pa_kernel(
             return table.rearrange("p r (j t g) -> p (r j) t g", t=COMPONENTS, g=GAUSS)
 
         var_in = state_in[:, 0]
-        nc.scalar.activation(
-            out=as_jtg(tabs[:, INV_E1]), in_=over_components(var_in, ROW_TILES), func=ACT.Exp, scale=-2.0
-        )
         nc.scalar.activation(out=unused_col[:], in_=one_col[:], func=ACT.Sigmoid)
-        nc.vector.tensor_scalar(
-            out=as_jtg(tabs[:, 0:2].rearrange("p w r c -> p (w r) c")),
-            in0=over_components(state_in[:].rearrange("p w r c -> p (w r) c"), 2 * ROW_TILES),
-            scalar1=1.0,
-            scalar2=None,
-            op0=ALU.add,
-        )
-        nc.vector.tensor_copy(
-            out=rep[:].rearrange("p w r (i c) -> p (w r) i c", i=2),
-            in_=tabs[:].rearrange("p w r c -> p (w r) c").unsqueeze(2).to_broadcast([P, 3 * ROW_TILES, 2, TABLE]),
-        )
+        nc.scalar.dma_start(out=weight_in[:], in_=s_weight_view)
+        nc.scalar.activation(out=sig_minus[:], in_=var_in, func=ACT.Sigmoid, scale=-2.0)
+        nc.scalar.activation(out=sig_plus[:], in_=var_in, func=ACT.Sigmoid, scale=2.0)
+
+        def widen_tables():
+            nc.vector.tensor_scalar(
+                out=as_jtg(tabs[:, 0:2].rearrange("p w r c -> p (w r) c")),
+                in0=over_components(state_in[:].rearrange("p w r c -> p (w r) c"), 2 * ROW_TILES),
+                scalar1=1.0,
+                scalar2=None,
+                op0=ALU.add,
+            )
+            nc.vector.reciprocal(out=inv_plus[:], in_=sig_plus[:])
+            nc.vector.tensor_tensor(
+                out=as_jtg(tabs[:, INV_E1]),
+                in0=over_components(sig_minus[:], ROW_TILES),
+                in1=over_components(inv_plus[:], ROW_TILES),
+                op=ALU.mult,
+            )
+            for i in range(3):
+                nc.vector.tensor_copy(
+                    out=rep[:, i].rearrange("p r (i c) -> p r i c", i=2),
+                    in_=tabs[:, i].unsqueeze(2).to_broadcast([P, ROW_TILES, 2, TABLE]),
+                )
 
         nc.gpsimd.tensor_copy(out=as_jtg(v1_tab[:]), in_=over_components(var_in, ROW_TILES))
         var_pairs = var_in.rearrange("p r (j g) -> p (r j) g", g=GAUSS)
@@ -222,11 +235,15 @@ def tile_chainlveg_pa_kernel(
                     )
             return xt
 
-        def regroup(r, xt):
-            nc.vector.tensor_copy(
+        def regroup(copy, r, xt):
+            copy(
                 out=grouped_words[:, :, 2 * P * r : 2 * P * (r + 1)].rearrange("p g (m u) -> p g m u", u=2),
                 in_=xt[:].rearrange("p (g u) m -> p g m u", u=2),
             )
+
+        def turn_table(i):
+            for r in range(ROW_TILES):
+                nc.tensor.transpose(turned[i][:, rows(r)], rep[:, i, r, :], ident[:])
 
         def quantise(g, lo, hi):
             nc.vector.quantize_mx(
@@ -235,20 +252,20 @@ def tile_chainlveg_pa_kernel(
                 in_=grouped[:, g, 4 * lo : 4 * hi],
             )
 
-        xts = [transpose_rows(r) for r in range(ROW_TILES)]
+        xt0 = transpose_rows(0)
+        regroup(nc.vector.tensor_copy, 0, xt0)
+        xt1 = transpose_rows(1)
+        regroup(nc.vector.tensor_copy, 1, xt1)
         bias_t = bank_ps.tile([P, P], BF16, name="bias_t", tag="bank")
         nc.tensor.transpose(bias_t[:], bias_rows[:], ident_bf[:])
         nc.scalar.activation(out=bias1[:], in_=bias_t[:, 0 : 2 * COL_TILES], func=ACT.Identity, bias=one_col[:])
-        regroup(0, xts[0])
-        regroup(1, xts[1])
-        for i in range(3):
-            for r in range(ROW_TILES):
-                nc.tensor.transpose(turned[i][:, rows(r)], rep[:, i, r, :], ident[:])
+        xt2 = transpose_rows(2)
         quantise(0, 0, 256)
-        regroup(2, xts[2])
+        regroup(nc.vector.tensor_copy, 2, xt2)
         quantise(1, 0, 256)
         quantise(0, 256, 384)
         quantise(1, 256, 384)
+        widen_tables()
 
         def project(w, k):
             for a in range(k * PER_GROUP, (k + 1) * PER_GROUP):
@@ -389,6 +406,8 @@ def tile_chainlveg_pa_kernel(
         mu_banks = [None, None]
         for k in range(GROUPS):
             project(LOGSTD, k)
+            if k == 0:
+                turn_table(LOGSTD)
             if k > 0:
                 sigmoid(k - 1)
             minus_state(LOGSTD, k)
@@ -398,6 +417,9 @@ def tile_chainlveg_pa_kernel(
             if k == 1:
                 finish_quad(0)
             project(MEAN, k)
+            if k == 0:
+                turn_table(MEAN)
+                turn_table(INV_E1)
             if k == 2:
                 mu_banks[0] = new_banks()
                 turn_back(d_share, 0, mu_banks[0])

@@ -335,17 +335,18 @@ def tile_chainlveg_pa_kernel(
         def for_each_label(table, r, width, n_labels):
             return table[:, r, :].unsqueeze(1).to_broadcast([P, n_labels, width])
 
-        def finish_mu(h, banks):
+        def finish_mu(h, banks, lo, hi, store):
             for r in range(ROW_TILES):
                 nc.vector.scalar_tensor_tensor(
-                    out=by_label(mu_sb[:, r, cols(h)], TABLE),
-                    in0=by_label(banks[r][:], TABLE),
+                    out=by_label(mu_sb[:, r, h * BANK + lo : h * BANK + hi], TABLE),
+                    in0=by_label(banks[r][:, lo:hi], TABLE),
                     scalar=1.0,
-                    in1=for_each_label(tabs[:, MEAN], r, TABLE, BANK // TABLE),
+                    in1=for_each_label(tabs[:, MEAN], r, TABLE, (hi - lo) // TABLE),
                     op0=ALU.subtract,
                     op1=ALU.add,
                 )
-                nc.sync.dma_start(out=mu_out[:, r, cols(h)], in_=mu_sb[:, r, cols(h)])
+                if store:
+                    nc.sync.dma_start(out=mu_out[:, r, cols(h)], in_=mu_sb[:, r, cols(h)])
 
         def finish_var(h, banks):
             for r in range(ROW_TILES):
@@ -359,19 +360,18 @@ def tile_chainlveg_pa_kernel(
                 )
                 nc.sync.dma_start(out=var_out[:, r, cols(h)], in_=var_sb[:, r, cols(h)])
 
-        def turn_pairs(k, banks):
+        def turn_pairs(src, k, banks, first, last):
             for r in range(ROW_TILES):
                 for a in range(k * PER_GROUP, (k + 1) * PER_GROUP):
                     slot = a % (COL_TILES // HALVES)
-                    for src, first in ((quad, True), (log_share, False)):
-                        nc.tensor.matmul(
-                            out=banks[r][:, slot * P : (slot + 1) * P],
-                            lhsT=src[:, a, rows(r)],
-                            rhs=perm[:],
-                            start=first,
-                            stop=not first,
-                            is_transpose=True,
-                        )
+                    nc.tensor.matmul(
+                        out=banks[r][:, slot * P : (slot + 1) * P],
+                        lhsT=src[:, a, rows(r)],
+                        rhs=perm[:],
+                        start=(first and a % PER_GROUP == 0),
+                        stop=(last and a % PER_GROUP == PER_GROUP - 1),
+                        is_transpose=True,
+                    )
 
         def finish_scale(h, banks):
             half = slice(h * BANK // GAUSS, (h + 1) * BANK // GAUSS)
@@ -385,6 +385,8 @@ def tile_chainlveg_pa_kernel(
                     op0=ALU.mult,
                     op1=ALU.add,
                 )
+            for r in range(ROW_TILES):
+                by_g = banks[r][:].rearrange("p (s g c) -> p s g c", g=GAUSS, c=PAIRS)
                 nc.vector.scalar_tensor_tensor(
                     out=by_label(scale_sb[:, r, half], PAIRS),
                     in0=by_g[:, :, 1, :],
@@ -422,28 +424,45 @@ def tile_chainlveg_pa_kernel(
                 turn_table(INV_E1)
             if k == 2:
                 mu_banks[0] = new_banks()
-                turn_back(d_share, 0, mu_banks[0])
+            if k >= 2:
+                turn_back(d_share, k - 2, mu_banks[0])
             minus_state(MEAN, k)
+            if k >= 2:
+                finish_mu(0, mu_banks[0], (k - 2) * BANK // 2, (k - 1) * BANK // 2, k == 3)
         sigmoid(GROUPS - 1)
         d_over_e1(GROUPS - 1)
         d_times_share(GROUPS - 1)
         for k in range(1, GROUPS):
             finish_quad(k)
 
-        turn_back(d_share, 1, mu_banks[0])
-        finish_mu(0, mu_banks[0])
+        pair_banks = [new_banks(), None]
+        turn_pairs(quad, 0, pair_banks[0], True, False)
         mu_banks[1] = new_banks()
         turn_back(d_share, 2, mu_banks[1])
         turn_back(d_share, 3, mu_banks[1])
-        finish_mu(1, mu_banks[1])
-        for h in range(HALVES):
-            var_banks = new_banks()
-            for k in (2 * h, 2 * h + 1):
-                log_of_rest(k)
-                turn_back(log_rest, k, var_banks)
-            finish_var(h, var_banks)
-            pair_banks = new_banks()
-            for k in (2 * h, 2 * h + 1):
-                log_of_share(k)
-                turn_pairs(k, pair_banks)
-            finish_scale(h, pair_banks)
+        finish_mu(1, mu_banks[1], 0, BANK, True)
+        var_banks = new_banks()
+        for k in (0, 1):
+            log_of_rest(k)
+            turn_back(log_rest, k, var_banks)
+        finish_var(0, var_banks)
+        log_of_share(0)
+        turn_pairs(log_share, 0, pair_banks[0], False, False)
+        turn_pairs(quad, 1, pair_banks[0], False, False)
+        log_of_share(1)
+        turn_pairs(log_share, 1, pair_banks[0], False, True)
+        finish_scale(0, pair_banks[0])
+        var_banks = new_banks()
+        log_of_rest(2)
+        turn_back(log_rest, 2, var_banks)
+        pair_banks[1] = new_banks()
+        turn_pairs(quad, 2, pair_banks[1], True, False)
+        log_of_rest(3)
+        turn_back(log_rest, 3, var_banks)
+        finish_var(1, var_banks)
+        log_of_share(2)
+        turn_pairs(log_share, 2, pair_banks[1], False, False)
+        log_of_share(3)
+        turn_pairs(log_share, 3, pair_banks[1], False, False)
+        turn_pairs(quad, 3, pair_banks[1], False, True)
+        finish_scale(1, pair_banks[1])

@@ -127,8 +127,8 @@ def tile_chainlveg_pa_kernel(
 
         turned = [bank_ps.tile([P, ROWS], F32, name="turned%d" % i, tag="bank") for i in range(3)]
 
-        nc.vector.memset(bias_rows[:], 0.0)
         nc.vector.memset(one_col[:], 1.0)
+        nc.gpsimd.memset(bias_rows[:], 0.0)
         for w in range(2):
             nc.gpsimd.memset(w_planes[w][:].bitcast(F32), 0.0)
         make_identity(nc, ident[:])
@@ -150,19 +150,19 @@ def tile_chainlveg_pa_kernel(
 
         for r in range(ROW_TILES):
             nc.scalar.dma_start(out=x_sb[:, r, :], in_=x_view[:, r, :])
-        for w in (LOGSTD, MEAN):
-            nc.scalar.dma_start(
-                out=bias_rows[COL_TILES * w : COL_TILES * (w + 1), :],
-                in_=bias_in[w].rearrange("(a p) -> a p", p=P),
-            )
         nc.scalar.dma_start(out=state_in[:, 0], in_=s_var_view)
         nc.scalar.dma_start(out=state_in[:, 1], in_=s_mu_view)
         for w in (LOGSTD, MEAN):
+            nc.sync.dma_start(
+                out=bias_rows[COL_TILES * w : COL_TILES * (w + 1), :],
+                in_=bias_in[w].rearrange("(a p) -> a p", p=P),
+            )
+        for w in (LOGSTD, MEAN):
             load_scales(w)
-            load_words(w, 0, 256)
-        for lo, hi in ((256, 512), (512, 1024)):
-            for w in (LOGSTD, MEAN):
-                load_words(w, lo, hi)
+            load_words(w, 0, BANK)
+        for w in (LOGSTD, MEAN):
+            load_words(w, BANK, N)
+        nc.sync.dma_start(out=weight_in[:], in_=s_weight_view)
 
         def over_components(small, n_outer):
             pairs = small.rearrange("p r (j g) -> p (r j) g", g=GAUSS)
@@ -173,9 +173,10 @@ def tile_chainlveg_pa_kernel(
 
         var_in = state_in[:, 0]
         nc.scalar.activation(out=unused_col[:], in_=one_col[:], func=ACT.Sigmoid)
-        nc.scalar.dma_start(out=weight_in[:], in_=s_weight_view)
-        nc.scalar.activation(out=sig_minus[:], in_=var_in, func=ACT.Sigmoid, scale=-2.0)
-        nc.scalar.activation(out=sig_plus[:], in_=var_in, func=ACT.Sigmoid, scale=2.0)
+
+        def two_sigmoids():
+            nc.scalar.activation(out=sig_minus[:], in_=var_in, func=ACT.Sigmoid, scale=-2.0)
+            nc.scalar.activation(out=sig_plus[:], in_=var_in, func=ACT.Sigmoid, scale=2.0)
 
         def widen_tables():
             nc.vector.tensor_scalar(
@@ -185,14 +186,15 @@ def tile_chainlveg_pa_kernel(
                 scalar2=None,
                 op0=ALU.add,
             )
-            nc.vector.reciprocal(out=inv_plus[:], in_=sig_plus[:])
-            nc.vector.tensor_tensor(
-                out=as_jtg(tabs[:, INV_E1]),
-                in0=over_components(sig_minus[:], ROW_TILES),
-                in1=over_components(inv_plus[:], ROW_TILES),
-                op=ALU.mult,
-            )
             for i in range(3):
+                if i == INV_E1:
+                    nc.vector.reciprocal(out=inv_plus[:], in_=sig_plus[:])
+                    nc.vector.tensor_tensor(
+                        out=as_jtg(tabs[:, INV_E1]),
+                        in0=over_components(sig_minus[:], ROW_TILES),
+                        in1=over_components(inv_plus[:], ROW_TILES),
+                        op=ALU.mult,
+                    )
                 nc.vector.tensor_copy(
                     out=rep[:, i].rearrange("p r (i c) -> p r i c", i=2),
                     in_=tabs[:, i].unsqueeze(2).to_broadcast([P, ROW_TILES, 2, TABLE]),
@@ -259,6 +261,7 @@ def tile_chainlveg_pa_kernel(
         bias_t = bank_ps.tile([P, P], BF16, name="bias_t", tag="bank")
         nc.tensor.transpose(bias_t[:], bias_rows[:], ident_bf[:])
         nc.scalar.activation(out=bias1[:], in_=bias_t[:, 0 : 2 * COL_TILES], func=ACT.Identity, bias=one_col[:])
+        two_sigmoids()
         xt2 = transpose_rows(2)
         quantise(0, 0, 256)
         regroup(nc.vector.tensor_copy, 2, xt2)
@@ -375,27 +378,36 @@ def tile_chainlveg_pa_kernel(
 
         def finish_scale(h, banks):
             half = slice(h * BANK // GAUSS, (h + 1) * BANK // GAUSS)
-            for r in range(ROW_TILES):
-                by_g = banks[r][:].rearrange("p (s g c) -> p s g c", g=GAUSS, c=PAIRS)
+
+            def by_g(r, g):
+                return banks[r][:].rearrange("p (s g c) -> p s g c", g=GAUSS, c=PAIRS)[:, :, g, :]
+
+            def first_step(r):
                 nc.vector.scalar_tensor_tensor(
                     out=by_label(half_sum[:, r, half], PAIRS),
-                    in0=by_g[:, :, 0, :],
+                    in0=by_g(r, 0),
                     scalar=0.5,
                     in1=for_each_label(c_twice, r, PAIRS, COL_TILES // HALVES),
                     op0=ALU.mult,
                     op1=ALU.add,
                 )
-            for r in range(ROW_TILES):
-                by_g = banks[r][:].rearrange("p (s g c) -> p s g c", g=GAUSS, c=PAIRS)
+
+            def second_step(r):
                 nc.vector.scalar_tensor_tensor(
                     out=by_label(scale_sb[:, r, half], PAIRS),
-                    in0=by_g[:, :, 1, :],
+                    in0=by_g(r, 1),
                     scalar=0.5,
                     in1=by_label(half_sum[:, r, half], PAIRS),
                     op0=ALU.mult,
                     op1=ALU.add,
                 )
                 nc.sync.dma_start(out=scale_out[:, r, half], in_=scale_sb[:, r, half])
+
+            first_step(0)
+            for r in range(1, ROW_TILES):
+                first_step(r)
+                second_step(r - 1)
+            second_step(ROW_TILES - 1)
 
         def log_of_rest(k):
             nc.scalar.activation(
@@ -406,18 +418,13 @@ def tile_chainlveg_pa_kernel(
             nc.scalar.activation(out=log_share[:, group(k), :], in_=share[:, group(k), :], func=ACT.Ln)
 
         mu_banks = [None, None]
+        project(LOGSTD, 0)
+        turn_table(LOGSTD)
+        minus_state(LOGSTD, 0)
         for k in range(GROUPS):
-            project(LOGSTD, k)
-            if k == 0:
-                turn_table(LOGSTD)
-            if k > 0:
-                sigmoid(k - 1)
-            minus_state(LOGSTD, k)
-            if k > 0:
-                d_over_e1(k - 1)
-                d_times_share(k - 1)
-            if k == 1:
-                finish_quad(0)
+            if k + 1 < GROUPS:
+                project(LOGSTD, k + 1)
+                minus_state(LOGSTD, k + 1)
             project(MEAN, k)
             if k == 0:
                 turn_table(MEAN)
@@ -427,11 +434,13 @@ def tile_chainlveg_pa_kernel(
             if k >= 2:
                 turn_back(d_share, k - 2, mu_banks[0])
             minus_state(MEAN, k)
+            sigmoid(k)
+            d_over_e1(k)
+            d_times_share(k)
+            if k == 0:
+                finish_quad(0)
             if k >= 2:
                 finish_mu(0, mu_banks[0], (k - 2) * BANK // 2, (k - 1) * BANK // 2, k == 3)
-        sigmoid(GROUPS - 1)
-        d_over_e1(GROUPS - 1)
-        d_times_share(GROUPS - 1)
         for k in range(1, GROUPS):
             finish_quad(k)
 

@@ -101,9 +101,6 @@ def tile_chainlveg_pa_kernel(
         x_planes = keep.tile([P, PASSES, ROWS], U8, align_bytes=64)
         state_in = keep.tile([P, 2, ROW_TILES, STATE], BF16)
         weight_in = keep.tile([P, ROW_TILES, LABELS], BF16)
-        sig_minus = keep.tile([P, ROW_TILES, STATE], F32)
-        sig_plus = keep.tile([P, ROW_TILES, STATE], F32)
-        inv_plus = keep.tile([P, ROW_TILES, STATE], F32)
         v_sum = keep.tile([P, ROW_TILES * LABELS], F32)
         w_shift = keep.tile([P, ROW_TILES * LABELS], F32)
         tabs = keep.tile([P, 3, ROW_TILES, TABLE], F32)
@@ -172,33 +169,24 @@ def tile_chainlveg_pa_kernel(
             return table.rearrange("p r (j t g) -> p (r j) t g", t=COMPONENTS, g=GAUSS)
 
         var_in = state_in[:, 0]
+        nc.scalar.activation(out=unused_col[:], in_=one_col[:], func=ACT.Exp)
+        nc.scalar.activation(
+            out=as_jtg(tabs[:, INV_E1]), in_=over_components(var_in, ROW_TILES), func=ACT.Exp, scale=-2.0
+        )
         nc.scalar.activation(out=unused_col[:], in_=one_col[:], func=ACT.Sigmoid)
-
-        def two_sigmoids():
-            nc.scalar.activation(out=sig_minus[:], in_=var_in, func=ACT.Sigmoid, scale=-2.0)
-            nc.scalar.activation(out=sig_plus[:], in_=var_in, func=ACT.Sigmoid, scale=2.0)
-
-        def widen_tables():
-            nc.vector.tensor_scalar(
-                out=as_jtg(tabs[:, 0:2].rearrange("p w r c -> p (w r) c")),
-                in0=over_components(state_in[:].rearrange("p w r c -> p (w r) c"), 2 * ROW_TILES),
-                scalar1=1.0,
-                scalar2=None,
-                op0=ALU.add,
+        nc.gpsimd.tensor_scalar(
+            out=as_jtg(tabs[:, 0:2].rearrange("p w r c -> p (w r) c")),
+            in0=over_components(state_in[:].rearrange("p w r c -> p (w r) c"), 2 * ROW_TILES),
+            scalar1=1.0,
+            scalar2=1.0,
+            op0=ALU.mult,
+            op1=ALU.add,
+        )
+        for i in range(3):
+            nc.gpsimd.tensor_copy(
+                out=rep[:, i].rearrange("p r (i c) -> p r i c", i=2),
+                in_=tabs[:, i].unsqueeze(2).to_broadcast([P, ROW_TILES, 2, TABLE]),
             )
-            for i in range(3):
-                if i == INV_E1:
-                    nc.vector.reciprocal(out=inv_plus[:], in_=sig_plus[:])
-                    nc.vector.tensor_tensor(
-                        out=as_jtg(tabs[:, INV_E1]),
-                        in0=over_components(sig_minus[:], ROW_TILES),
-                        in1=over_components(inv_plus[:], ROW_TILES),
-                        op=ALU.mult,
-                    )
-                nc.vector.tensor_copy(
-                    out=rep[:, i].rearrange("p r (i c) -> p r i c", i=2),
-                    in_=tabs[:, i].unsqueeze(2).to_broadcast([P, ROW_TILES, 2, TABLE]),
-                )
 
         nc.gpsimd.tensor_copy(out=as_jtg(v1_tab[:]), in_=over_components(var_in, ROW_TILES))
         var_pairs = var_in.rearrange("p r (j g) -> p (r j) g", g=GAUSS)
@@ -261,14 +249,12 @@ def tile_chainlveg_pa_kernel(
         bias_t = bank_ps.tile([P, P], BF16, name="bias_t", tag="bank")
         nc.tensor.transpose(bias_t[:], bias_rows[:], ident_bf[:])
         nc.scalar.activation(out=bias1[:], in_=bias_t[:, 0 : 2 * COL_TILES], func=ACT.Identity, bias=one_col[:])
-        two_sigmoids()
         xt2 = transpose_rows(2)
-        quantise(0, 0, 256)
         regroup(nc.vector.tensor_copy, 2, xt2)
+        quantise(0, 0, 256)
         quantise(1, 0, 256)
         quantise(0, 256, 384)
         quantise(1, 256, 384)
-        widen_tables()
 
         def project(w, k):
             for a in range(k * PER_GROUP, (k + 1) * PER_GROUP):
@@ -439,8 +425,8 @@ def tile_chainlveg_pa_kernel(
             d_times_share(k)
             if k == 0:
                 finish_quad(0)
-            if k >= 2:
-                finish_mu(0, mu_banks[0], (k - 2) * BANK // 2, (k - 1) * BANK // 2, k == 3)
+            if k == 3:
+                finish_mu(0, mu_banks[0], 0, BANK, True)
         for k in range(1, GROUPS):
             finish_quad(k)
 

@@ -157,9 +157,9 @@ def tile_chainlveg_pa_kernel(
         for w in (LOGSTD, MEAN):
             load_scales(w)
             load_words(w, 0, BANK)
+        nc.sync.dma_start(out=weight_in[:], in_=s_weight_view)
         for w in (LOGSTD, MEAN):
             load_words(w, BANK, N)
-        nc.sync.dma_start(out=weight_in[:], in_=s_weight_view)
 
         def over_components(small, n_outer):
             pairs = small.rearrange("p r (j g) -> p (r j) g", g=GAUSS)
@@ -174,44 +174,57 @@ def tile_chainlveg_pa_kernel(
             out=as_jtg(tabs[:, INV_E1]), in_=over_components(var_in, ROW_TILES), func=ACT.Exp, scale=-2.0
         )
         nc.scalar.activation(out=unused_col[:], in_=one_col[:], func=ACT.Sigmoid)
-        nc.gpsimd.tensor_scalar(
-            out=as_jtg(tabs[:, 0:2].rearrange("p w r c -> p (w r) c")),
-            in0=over_components(state_in[:].rearrange("p w r c -> p (w r) c"), 2 * ROW_TILES),
-            scalar1=1.0,
-            scalar2=1.0,
-            op0=ALU.mult,
-            op1=ALU.add,
-        )
-        for i in range(3):
+        def double_table(i):
             nc.gpsimd.tensor_copy(
                 out=rep[:, i].rearrange("p r (i c) -> p r i c", i=2),
                 in_=tabs[:, i].unsqueeze(2).to_broadcast([P, ROW_TILES, 2, TABLE]),
             )
 
-        nc.gpsimd.tensor_copy(out=as_jtg(v1_tab[:]), in_=over_components(var_in, ROW_TILES))
-        var_pairs = var_in.rearrange("p r (j g) -> p (r j) g", g=GAUSS)
-        nc.gpsimd.tensor_tensor(out=v_sum[:], in0=var_pairs[:, :, 0], in1=var_pairs[:, :, 1], op=ALU.add)
         nc.gpsimd.tensor_scalar(
-            out=w_shift[:],
-            in0=weight_in[:].rearrange("p r j -> p (r j)"),
-            scalar1=LOG_2PI,
-            scalar2=None,
-            op0=ALU.subtract,
+            out=as_jtg(tabs[:, LOGSTD]),
+            in0=over_components(var_in, ROW_TILES),
+            scalar1=1.0,
+            scalar2=1.0,
+            op0=ALU.mult,
+            op1=ALU.add,
         )
-        both = [P, ROW_TILES * LABELS, COMPONENTS]
-        nc.gpsimd.tensor_tensor(
-            out=c_tab[:].rearrange("p r (j t) -> p (r j) t", t=COMPONENTS),
-            in0=w_shift[:].unsqueeze(2).to_broadcast(both),
-            in1=v_sum[:].unsqueeze(2).to_broadcast(both),
-            op=ALU.subtract,
-        )
-        nc.gpsimd.tensor_copy(
-            out=c_twice[:].rearrange("p r (i c) -> p r i c", i=2),
-            in_=c_tab[:].unsqueeze(2).to_broadcast([P, ROW_TILES, 2, HALF_TABLE]),
-        )
-        nc.gpsimd.tensor_copy(
-            out=perm[:].rearrange("p (g c) -> p g c", g=GAUSS), in_=ident[:].rearrange("p (c g) -> p g c", g=GAUSS)
-        )
+        double_table(LOGSTD)
+
+        def other_tables():
+            nc.vector.tensor_scalar(
+                out=as_jtg(tabs[:, MEAN]),
+                in0=over_components(state_in[:, 1], ROW_TILES),
+                scalar1=1.0,
+                scalar2=None,
+                op0=ALU.add,
+            )
+            double_table(MEAN)
+            double_table(INV_E1)
+            nc.gpsimd.tensor_copy(out=as_jtg(v1_tab[:]), in_=over_components(var_in, ROW_TILES))
+            var_pairs = var_in.rearrange("p r (j g) -> p (r j) g", g=GAUSS)
+            nc.gpsimd.tensor_tensor(out=v_sum[:], in0=var_pairs[:, :, 0], in1=var_pairs[:, :, 1], op=ALU.add)
+            nc.gpsimd.tensor_scalar(
+                out=w_shift[:],
+                in0=weight_in[:].rearrange("p r j -> p (r j)"),
+                scalar1=LOG_2PI,
+                scalar2=None,
+                op0=ALU.subtract,
+            )
+            both = [P, ROW_TILES * LABELS, COMPONENTS]
+            nc.gpsimd.tensor_tensor(
+                out=c_tab[:].rearrange("p r (j t) -> p (r j) t", t=COMPONENTS),
+                in0=w_shift[:].unsqueeze(2).to_broadcast(both),
+                in1=v_sum[:].unsqueeze(2).to_broadcast(both),
+                op=ALU.subtract,
+            )
+            nc.gpsimd.tensor_copy(
+                out=c_twice[:].rearrange("p r (i c) -> p r i c", i=2),
+                in_=c_tab[:].unsqueeze(2).to_broadcast([P, ROW_TILES, 2, HALF_TABLE]),
+            )
+            nc.gpsimd.tensor_copy(
+                out=perm[:].rearrange("p (g c) -> p g c", g=GAUSS),
+                in_=ident[:].rearrange("p (c g) -> p g c", g=GAUSS),
+            )
 
         x_words = x_sb[:].bitcast(F32)
         grouped_words = grouped[:].bitcast(F32)
@@ -255,6 +268,7 @@ def tile_chainlveg_pa_kernel(
         quantise(1, 0, 256)
         quantise(0, 256, 384)
         quantise(1, 256, 384)
+        other_tables()
 
         def project(w, k):
             for a in range(k * PER_GROUP, (k + 1) * PER_GROUP):

@@ -418,8 +418,8 @@ def tile_chainlveg_pa_kernel(
             nc.scalar.activation(out=log_share[:, group(k), :], in_=share[:, group(k), :], func=ACT.Ln)
 
         mu_banks = [None, None]
-        project(LOGSTD, 0)
         turn_table(LOGSTD)
+        project(LOGSTD, 0)
         minus_state(LOGSTD, 0)
         for k in range(GROUPS):
             if k + 1 < GROUPS:
@@ -429,10 +429,10 @@ def tile_chainlveg_pa_kernel(
             if k == 0:
                 turn_table(MEAN)
                 turn_table(INV_E1)
-            if k == 2:
+            if k == 3:
                 mu_banks[0] = new_banks()
-            if k >= 2:
-                turn_back(d_share, k - 2, mu_banks[0])
+                turn_back(d_share, 0, mu_banks[0])
+                turn_back(d_share, 1, mu_banks[0])
             minus_state(MEAN, k)
             sigmoid(k)
             d_over_e1(k)

@@ -146,11 +146,11 @@ def tile_chainlveg_pa_kernel(
             )
 
         for r in range(ROW_TILES):
-            nc.scalar.dma_start(out=x_sb[:, r, :], in_=x_view[:, r, :])
+            nc.sync.dma_start(out=x_sb[:, r, :], in_=x_view[:, r, :])
         nc.scalar.dma_start(out=state_in[:, 0], in_=s_var_view)
         nc.scalar.dma_start(out=state_in[:, 1], in_=s_mu_view)
         for w in (LOGSTD, MEAN):
-            nc.sync.dma_start(
+            nc.scalar.dma_start(
                 out=bias_rows[COL_TILES * w : COL_TILES * (w + 1), :],
                 in_=bias_in[w].rearrange("(a p) -> a p", p=P),
             )

@@ -125,11 +125,15 @@ def tile_chainlveg_pa_kernel(
         turned = [bank_ps.tile([P, ROWS], F32, name="turned%d" % i, tag="bank") for i in range(3)]
 
         nc.vector.memset(one_col[:], 1.0)
-        nc.gpsimd.memset(bias_rows[:], 0.0)
         for w in range(2):
-            nc.gpsimd.memset(w_planes[w][:].bitcast(F32), 0.0)
+            nc.vector.memset(w_planes[w][:].bitcast(I32), 0)
+        nc.vector.memset(bias_rows[:], 0.0)
         make_identity(nc, ident[:])
-        make_identity(nc, ident_bf[:])
+        nc.vector.tensor_copy(out=ident_bf[:], in_=ident[:])
+        nc.vector.tensor_copy(
+            out=perm[:].rearrange("p (g c) -> p g c", g=GAUSS),
+            in_=ident[:].rearrange("p (c g) -> p g c", g=GAUSS),
+        )
 
         def load_scales(w):
             for quadrant in range(4):
@@ -175,18 +179,17 @@ def tile_chainlveg_pa_kernel(
         )
         nc.scalar.activation(out=unused_col[:], in_=one_col[:], func=ACT.Sigmoid)
         def double_table(i):
-            nc.gpsimd.tensor_copy(
+            nc.vector.tensor_copy(
                 out=rep[:, i].rearrange("p r (i c) -> p r i c", i=2),
                 in_=tabs[:, i].unsqueeze(2).to_broadcast([P, ROW_TILES, 2, TABLE]),
             )
 
-        nc.gpsimd.tensor_scalar(
+        nc.vector.tensor_scalar(
             out=as_jtg(tabs[:, LOGSTD]),
             in0=over_components(var_in, ROW_TILES),
             scalar1=1.0,
-            scalar2=1.0,
-            op0=ALU.mult,
-            op1=ALU.add,
+            scalar2=None,
+            op0=ALU.add,
         )
         double_table(LOGSTD)
 
@@ -220,10 +223,6 @@ def tile_chainlveg_pa_kernel(
             nc.gpsimd.tensor_copy(
                 out=c_twice[:].rearrange("p r (i c) -> p r i c", i=2),
                 in_=c_tab[:].unsqueeze(2).to_broadcast([P, ROW_TILES, 2, HALF_TABLE]),
-            )
-            nc.gpsimd.tensor_copy(
-                out=perm[:].rearrange("p (g c) -> p g c", g=GAUSS),
-                in_=ident[:].rearrange("p (c g) -> p g c", g=GAUSS),
             )
 
         x_words = x_sb[:].bitcast(F32)

@@ -433,13 +433,13 @@ def tile_chainlveg_pa_kernel(
                 turn_back(d_share, 0, mu_banks[0])
                 turn_back(d_share, 1, mu_banks[0])
             minus_state(MEAN, k)
+            if k == 3:
+                finish_mu(0, mu_banks[0], 0, BANK, True)
             sigmoid(k)
             d_over_e1(k)
             d_times_share(k)
             if k == 0:
                 finish_quad(0)
-            if k == 3:
-                finish_mu(0, mu_banks[0], 0, BANK, True)
         for k in range(1, GROUPS):
             finish_quad(k)
 

@@ -27,6 +27,7 @@ COL_TILES = N // P
 GROUPS = 4
 PER_GROUP = COL_TILES // GROUPS
 BANK = 512
+WARM_MATMULS = 3
 HALVES = N // BANK
 STATE = LABELS * GAUSS
 TABLE = LABELS * COMPONENTS * GAUSS
@@ -93,6 +94,7 @@ def tile_chainlveg_pa_kernel(
         bias_rows = keep.tile([P, P], BF16)
         bias1 = keep.tile([P, 2 * COL_TILES], F32)
         one_col = keep.tile([P, 1], F32)
+        zeros = keep.tile([P, BANK], BF16)
         unused_col = keep.tile([P, 1], F32)
         w_words = keep.tile([P, 2, PASSES, N], U32, align_bytes=64)
         w_planes = [keep.tile([P, N], U8, name="w_planes%d" % w, align_bytes=64) for w in range(2)]
@@ -124,6 +126,10 @@ def tile_chainlveg_pa_kernel(
 
         turned = [bank_ps.tile([P, ROWS], F32, name="turned%d" % i, tag="bank") for i in range(3)]
 
+        nc.vector.memset(zeros[:].bitcast(I32), 0)
+        warm = bank_ps.tile([P, BANK], F32, name="warm", tag="bank")
+        for _ in range(WARM_MATMULS):
+            nc.tensor.matmul(out=warm[:], lhsT=zeros[:, 0:P], rhs=zeros[:], start=True, stop=True)
         nc.vector.memset(one_col[:], 1.0)
         for w in range(2):
             nc.vector.memset(w_planes[w][:].bitcast(I32), 0)
@@ -159,8 +165,8 @@ def tile_chainlveg_pa_kernel(
                 in_=bias_in[w].rearrange("(a p) -> a p", p=P),
             )
         for w in (LOGSTD, MEAN):
-            load_scales(w)
             load_words(w, 0, BANK)
+            load_scales(w)
         nc.sync.dma_start(out=weight_in[:], in_=s_weight_view)
         for w in (LOGSTD, MEAN):
             load_words(w, BANK, N)
@@ -258,9 +264,6 @@ def tile_chainlveg_pa_kernel(
         regroup(nc.vector.tensor_copy, 0, xt0)
         xt1 = transpose_rows(1)
         regroup(nc.vector.tensor_copy, 1, xt1)
-        bias_t = bank_ps.tile([P, P], BF16, name="bias_t", tag="bank")
-        nc.tensor.transpose(bias_t[:], bias_rows[:], ident_bf[:])
-        nc.scalar.activation(out=bias1[:], in_=bias_t[:, 0 : 2 * COL_TILES], func=ACT.Identity, bias=one_col[:])
         xt2 = transpose_rows(2)
         regroup(nc.vector.tensor_copy, 2, xt2)
         quantise(0, 0, 256)
@@ -418,6 +421,9 @@ def tile_chainlveg_pa_kernel(
 
         mu_banks = [None, None]
         turn_table(LOGSTD)
+        bias_t = bank_ps.tile([P, P], BF16, name="bias_t", tag="bank")
+        nc.tensor.transpose(bias_t[:], bias_rows[:], ident_bf[:])
+        nc.scalar.activation(out=bias1[:], in_=bias_t[:, 0 : 2 * COL_TILES], func=ACT.Identity, bias=one_col[:])
         project(LOGSTD, 0)
         minus_state(LOGSTD, 0)
         for k in range(GROUPS):

@@ -126,6 +126,7 @@ def tile_chainlveg_pa_kernel(
 
         turned = [bank_ps.tile([P, ROWS], F32, name="turned%d" % i, tag="bank") for i in range(3)]
 
+        nc.vector.memset(bias_rows[:], 0.0)
         nc.vector.memset(zeros[:].bitcast(I32), 0)
         warm = bank_ps.tile([P, BANK], F32, name="warm", tag="bank")
         for _ in range(WARM_MATMULS):
@@ -133,7 +134,6 @@ def tile_chainlveg_pa_kernel(
         nc.vector.memset(one_col[:], 1.0)
         for w in range(2):
             nc.vector.memset(w_planes[w][:].bitcast(I32), 0)
-        nc.vector.memset(bias_rows[:], 0.0)
         make_identity(nc, ident[:])
         nc.vector.tensor_copy(out=ident_bf[:], in_=ident[:])
         nc.vector.tensor_copy(
@@ -302,6 +302,18 @@ def tile_chainlveg_pa_kernel(
                 out=t, in0=t, scalar=2.0, in1=for_each_tile(turned[w]), op0=ALU.min, op1=ALU.subtract
             )
 
+        def minus_state_tile(w, a):
+            t = proj[w][:, a, :]
+            nc.vector.scalar_tensor_tensor(
+                out=t, in0=t, scalar=2.0, in1=turned[w][:], op0=ALU.min, op1=ALU.subtract
+            )
+
+        def sigmoid_tile(a):
+            nc.scalar.activation(out=share[:, a, :], in_=share[:, a, :], func=ACT.Sigmoid, scale=-2.0)
+
+        def d_times_share_tile(a):
+            nc.gpsimd.tensor_tensor(out=d_share[:, a, :], in0=d[:, a, :], in1=share[:, a, :], op=ALU.mult)
+
         def sigmoid(k):
             nc.scalar.activation(out=share[:, group(k), :], in_=share[:, group(k), :], func=ACT.Sigmoid, scale=-2.0)
 
@@ -425,31 +437,42 @@ def tile_chainlveg_pa_kernel(
         nc.tensor.transpose(bias_t[:], bias_rows[:], ident_bf[:])
         nc.scalar.activation(out=bias1[:], in_=bias_t[:, 0 : 2 * COL_TILES], func=ACT.Identity, bias=one_col[:])
         project(LOGSTD, 0)
-        minus_state(LOGSTD, 0)
-        for k in range(GROUPS):
-            if k + 1 < GROUPS:
-                project(LOGSTD, k + 1)
-                minus_state(LOGSTD, k + 1)
+        for a in range(PER_GROUP):
+            minus_state_tile(LOGSTD, a)
+        project(MEAN, 0)
+        turn_table(MEAN)
+        for a in range(PER_GROUP):
+            minus_state_tile(MEAN, a)
+        for a in range(PER_GROUP):
+            sigmoid_tile(a)
+        for a in range(PER_GROUP):
+            d_times_share_tile(a)
+        turn_table(INV_E1)
+        d_over_e1(0)
+        finish_quad(0)
+        project(LOGSTD, 1)
+        minus_state(LOGSTD, 1)
+        for k in range(1, GROUPS):
             project(MEAN, k)
-            if k == 0:
-                turn_table(MEAN)
-                turn_table(INV_E1)
             if k == 3:
                 mu_banks[0] = new_banks()
                 turn_back(d_share, 0, mu_banks[0])
                 turn_back(d_share, 1, mu_banks[0])
             minus_state(MEAN, k)
+            if k + 1 < GROUPS:
+                project(LOGSTD, k + 1)
+                minus_state(LOGSTD, k + 1)
             if k == 3:
                 finish_mu(0, mu_banks[0], 0, BANK, True)
             sigmoid(k)
             d_over_e1(k)
             d_times_share(k)
-            if k == 0:
-                finish_quad(0)
         for k in range(1, GROUPS):
             finish_quad(k)
 
         pair_banks = [new_banks(), None]
+        for r in range(2):
+            nc.tensor.matmul(out=pair_banks[0][r][:], lhsT=zeros[:, 0:P], rhs=zeros[:], start=True, stop=True)
         turn_pairs(quad, 0, pair_banks[0], True, False)
         mu_banks[1] = new_banks()
         turn_back(d_share, 2, mu_banks[1])

import math
from contextlib import ExitStack

import concourse.mybir as mybir
from concourse.masks import make_identity

F32 = mybir.dt.float32
BF16 = mybir.dt.bfloat16
I32 = mybir.dt.int32
U32 = mybir.dt.uint32
U8 = mybir.dt.uint8
FP8X4 = mybir.dt.float8_e4m3fn_x4
ALU = mybir.AluOpType
ACT = mybir.ActivationFunctionType

P = 128
ROWS = 2 * 192
ROW_TILES = ROWS // P
K = 1024
K_PASS = 4 * P
PASSES = K // K_PASS
LABELS = 16
COMPONENTS = 2
GAUSS = 2
N = LABELS * LABELS * COMPONENTS * GAUSS
COL_TILES = N // P
GROUPS = 4
PER_GROUP = COL_TILES // GROUPS
BANK = 512
WARM_MATMULS = 3
HALVES = N // BANK
STATE = LABELS * GAUSS
TABLE = LABELS * COMPONENTS * GAUSS
HALF_TABLE = LABELS * COMPONENTS
PAIRS = P // GAUSS
LOG_2PI = math.log(2.0 * math.pi)
LOGSTD = 0
MEAN = 1
INV_E1 = 2
ROW_SPLITS = ((0, 256), (256, 384))

FLOPS = 2 * ROWS * K * 2 * N


def tile_chainlveg_pa_kernel(
    tc,
    x,
    s_weight,
    s_mu,
    s_var,
    tcm_w_words,
    tcm_w_scales,
    tcm_b,
    tcv_w_words,
    tcv_w_scales,
    tcv_b,
    out_0,
    out_1,
    out_2,
):
    nc = tc.nc
    words_in = [tcv_w_words, tcm_w_words]
    scales_in = [tcv_w_scales, tcm_w_scales]
    bias_in = [tcv_b, tcm_b]

    def by_row_tile(flat):
        return flat.rearrange("(p r) c -> p r c", r=ROW_TILES)

    x_view = by_row_tile(x.flatten_outer_dims())
    s_mu_view = by_row_tile(s_mu.rearrange("b q j e g -> (b q) (j e g)"))
    s_var_view = by_row_tile(s_var.rearrange("b q j e g -> (b q) (j e g)"))
    s_weight_view = by_row_tile(s_weight.rearrange("b q j e -> (b q) (j e)"))
    scale_out = by_row_tile(out_0.rearrange("b q i j t e -> (b q) (i j t e)"))
    mu_out = by_row_tile(out_1.rearrange("b q i j t e g -> (b q) (i j t e g)"))
    var_out = by_row_tile(out_2.rearrange("b q i j t e g -> (b q) (i j t e g)"))

    def cols(h):
        return slice(h * BANK, (h + 1) * BANK)

    def rows(r):
        return slice(r * P, (r + 1) * P)

    def group(k):
        return slice(k * PER_GROUP, (k + 1) * PER_GROUP)

    with ExitStack() as ctx:
        keep = ctx.enter_context(tc.tile_pool(name="keep", bufs=1))
        bank_ps = ctx.enter_context(tc.psum_pool(name="bank_ps", bufs=8))
        ctx.enter_context(tc.manual_schedule())

        x_sb = keep.tile([P, ROW_TILES, K], BF16)
        ident = keep.tile([P, P], F32)
        ident_bf = keep.tile([P, P], BF16)
        bias_rows = keep.tile([P, P], BF16)
        bias1 = keep.tile([P, 2 * COL_TILES], F32)
        one_col = keep.tile([P, 1], F32)
        zeros = keep.tile([P, BANK], BF16)
        unused_col = keep.tile([P, 1], F32)
        w_words = keep.tile([P, 2, PASSES, N], U32, align_bytes=64)
        w_planes = [keep.tile([P, N], U8, name="w_planes%d" % w, align_bytes=64) for w in range(2)]
        grouped = keep.tile([P, PASSES, 4 * ROWS], BF16, align_bytes=64)
        x_codes = keep.tile([P, PASSES, ROWS], U32, align_bytes=64)
        x_planes = keep.tile([P, PASSES, ROWS], U8, align_bytes=64)
        state_in = keep.tile([P, 2, ROW_TILES, STATE], BF16)
        weight_in = keep.tile([P, ROW_TILES, LABELS], BF16)
        v_sum = keep.tile([P, ROW_TILES * LABELS], F32)
        w_shift = keep.tile([P, ROW_TILES * LABELS], F32)
        tabs = keep.tile([P, 3, ROW_TILES, TABLE], F32)
        rep = keep.tile([P, 3, ROW_TILES, 2 * TABLE], F32)
        v1_tab = keep.tile([P, ROW_TILES, TABLE], F32)
        c_tab = keep.tile([P, ROW_TILES, HALF_TABLE], F32)
        c_twice = keep.tile([P, ROW_TILES, 2 * HALF_TABLE], F32)
        perm = keep.tile([P, P], F32)
        half_sum = keep.tile([P, ROW_TILES, N // GAUSS], F32)

        share = keep.tile([P, COL_TILES, ROWS], F32)
        d = keep.tile([P, COL_TILES, ROWS], F32)
        d_share = keep.tile([P, COL_TILES, ROWS], F32)
        quad = keep.tile([P, COL_TILES, ROWS], F32)
        log_share = keep.tile([P, COL_TILES, ROWS], F32)
        log_rest = keep.tile([P, COL_TILES, ROWS], F32)
        proj = [share, d]
        mu_sb = keep.tile([P, ROW_TILES, N], F32)
        var_sb = keep.tile([P, ROW_TILES, N], F32)
        scale_sb = keep.tile([P, ROW_TILES, N // GAUSS], F32)

        turned = [bank_ps.tile([P, ROWS], F32, name="turned%d" % i, tag="bank") for i in range(3)]

        nc.vector.memset(bias_rows[:], 0.0)
        nc.vector.memset(zeros[:].bitcast(I32), 0)
        warm = bank_ps.tile([P, BANK], F32, name="warm", tag="bank")
        for _ in range(WARM_MATMULS):
            nc.tensor.matmul(out=warm[:], lhsT=zeros[:, 0:P], rhs=zeros[:], start=True, stop=True)
        nc.vector.memset(one_col[:], 1.0)
        for w in range(2):
            nc.vector.memset(w_planes[w][:].bitcast(I32), 0)
        make_identity(nc, ident[:])
        nc.vector.tensor_copy(out=ident_bf[:], in_=ident[:])
        nc.vector.tensor_copy(
            out=perm[:].rearrange("p (g c) -> p g c", g=GAUSS),
            in_=ident[:].rearrange("p (c g) -> p g c", g=GAUSS),
        )

        def load_scales(w):
            for quadrant in range(4):
                nc.sync.dma_start(
                    out=w_planes[w][32 * quadrant : 32 * quadrant + 4 * PASSES, :].bitcast(I32),
                    in_=scales_in[w][:, 4 * quadrant : 4 * quadrant + 4, :].bitcast(I32),
                )

        def load_words(w, lo, hi):
            by_partition = words_in[w].rearrange("g p n t -> p g (n t)")
            nc.sync.dma_start(
                out=w_words[:, w, :, lo:hi].bitcast(I32),
                in_=by_partition[:, :, 4 * lo : 4 * hi].bitcast(I32),
            )

        for r in range(ROW_TILES):
            nc.sync.dma_start(out=x_sb[:, r, :], in_=x_view[:, r, :])
        nc.scalar.dma_start(out=state_in[:, 0], in_=s_var_view)
        nc.scalar.dma_start(out=state_in[:, 1], in_=s_mu_view)
        for w in (LOGSTD, MEAN):
            nc.scalar.dma_start(
                out=bias_rows[COL_TILES * w : COL_TILES * (w + 1), :],
                in_=bias_in[w].rearrange("(a p) -> a p", p=P),
            )
        for w in (LOGSTD, MEAN):
            load_words(w, 0, BANK)
            load_scales(w)
        nc.sync.dma_start(out=weight_in[:], in_=s_weight_view)
        for w in (LOGSTD, MEAN):
            load_words(w, BANK, N)

        def over_components(small, n_outer):
            pairs = small.rearrange("p r (j g) -> p (r j) g", g=GAUSS)
            return pairs.unsqueeze(2).to_broadcast([P, n_outer * LABELS, COMPONENTS, GAUSS])

        def as_jtg(table):
            return table.rearrange("p r (j t g) -> p (r j) t g", t=COMPONENTS, g=GAUSS)

        var_in = state_in[:, 0]
        nc.scalar.activation(out=unused_col[:], in_=one_col[:], func=ACT.Exp)
        nc.scalar.activation(
            out=as_jtg(tabs[:, INV_E1]), in_=over_components(var_in, ROW_TILES), func=ACT.Exp, scale=-2.0
        )
        nc.scalar.activation(out=unused_col[:], in_=one_col[:], func=ACT.Sigmoid)
        def double_table(i):
            nc.vector.tensor_copy(
                out=rep[:, i].rearrange("p r (i c) -> p r i c", i=2),
                in_=tabs[:, i].unsqueeze(2).to_broadcast([P, ROW_TILES, 2, TABLE]),
            )

        nc.vector.tensor_scalar(
            out=as_jtg(tabs[:, LOGSTD]),
            in0=over_components(var_in, ROW_TILES),
            scalar1=1.0,
            scalar2=None,
            op0=ALU.add,
        )
        double_table(LOGSTD)

        def other_tables():
            nc.vector.tensor_scalar(
                out=as_jtg(tabs[:, MEAN]),
                in0=over_components(state_in[:, 1], ROW_TILES),
                scalar1=1.0,
                scalar2=None,
                op0=ALU.add,
            )
            double_table(MEAN)
            double_table(INV_E1)
            nc.gpsimd.tensor_copy(out=as_jtg(v1_tab[:]), in_=over_components(var_in, ROW_TILES))
            var_pairs = var_in.rearrange("p r (j g) -> p (r j) g", g=GAUSS)
            nc.gpsimd.tensor_tensor(out=v_sum[:], in0=var_pairs[:, :, 0], in1=var_pairs[:, :, 1], op=ALU.add)
            nc.gpsimd.tensor_scalar(
                out=w_shift[:],
                in0=weight_in[:].rearrange("p r j -> p (r j)"),
                scalar1=LOG_2PI,
                scalar2=None,
                op0=ALU.subtract,
            )
            both = [P, ROW_TILES * LABELS, COMPONENTS]
            nc.gpsimd.tensor_tensor(
                out=c_tab[:].rearrange("p r (j t) -> p (r j) t", t=COMPONENTS),
                in0=w_shift[:].unsqueeze(2).to_broadcast(both),
                in1=v_sum[:].unsqueeze(2).to_broadcast(both),
                op=ALU.subtract,
            )
            nc.gpsimd.tensor_copy(
                out=c_twice[:].rearrange("p r (i c) -> p r i c", i=2),
                in_=c_tab[:].unsqueeze(2).to_broadcast([P, ROW_TILES, 2, HALF_TABLE]),
            )

        x_words = x_sb[:].bitcast(F32)
        grouped_words = grouped[:].bitcast(F32)

        def transpose_rows(r):
            xt = bank_ps.tile([P, 2 * PASSES, P], F32, name="xt", tag="bank")
            for g in range(PASSES):
                for u in range(2):
                    nc.tensor.transpose(
                        xt[:, 2 * g + u, :], x_words[:, r, 256 * g + u : 256 * (g + 1) : 2], ident[:]
                    )
            return xt

        def regroup(copy, r, xt):
            copy(
                out=grouped_words[:, :, 2 * P * r : 2 * P * (r + 1)].rearrange("p g (m u) -> p g m u", u=2),
                in_=xt[:].rearrange("p (g u) m -> p g m u", u=2),
            )

        def turn_table(i):
            for r in range(ROW_TILES):
                nc.tensor.transpose(turned[i][:, rows(r)], rep[:, i, r, :], ident[:])

        def quantise(g, lo, hi):
            nc.vector.quantize_mx(
                out=x_codes[:, g, lo:hi].bitcast(FP8X4),
                scales=x_planes[:, g, lo:hi],
                in_=grouped[:, g, 4 * lo : 4 * hi],
            )

        xt0 = transpose_rows(0)
        regroup(nc.vector.tensor_copy, 0, xt0)
        xt1 = transpose_rows(1)
        regroup(nc.vector.tensor_copy, 1, xt1)
        xt2 = transpose_rows(2)
        regroup(nc.vector.tensor_copy, 2, xt2)
        quantise(0, 0, 256)
        quantise(1, 0, 256)
        quantise(0, 256, 384)
        quantise(1, 256, 384)
        other_tables()

        def project(w, k):
            for a in range(k * PER_GROUP, (k + 1) * PER_GROUP):
                acc = bank_ps.tile([P, ROWS], F32, name="acc", tag="bank")
                for lo, hi in ROW_SPLITS:
                    for g in range(PASSES):
                        nc.tensor.matmul_mx(
                            out=acc[:, lo:hi],
                            lhsT=w_words[:, w, g, a * P : (a + 1) * P].bitcast(FP8X4),
                            lhsT_scale=w_planes[w][4 * g : P, a * P : (a + 1) * P],
                            rhs=x_codes[:, g, lo:hi].bitcast(FP8X4),
                            rhs_scale=x_planes[:, g, lo:hi],
                            start=(g == 0),
                            stop=(g == PASSES - 1),
                        )
                nc.scalar.activation(
                    out=proj[w][:, a, :],
                    in_=acc[:],
                    func=ACT.Relu,
                    bias=bias1[:, COL_TILES * w + a : COL_TILES * w + a + 1],
                )

        def for_each_tile(table):
            return table[:].unsqueeze(1).to_broadcast([P, PER_GROUP, ROWS])

        def minus_state(w, k):
            t = proj[w][:, group(k), :]
            nc.vector.scalar_tensor_tensor(
                out=t, in0=t, scalar=2.0, in1=for_each_tile(turned[w]), op0=ALU.min, op1=ALU.subtract
            )

        def minus_state_tile(w, a):
            t = proj[w][:, a, :]
            nc.vector.scalar_tensor_tensor(
                out=t, in0=t, scalar=2.0, in1=turned[w][:], op0=ALU.min, op1=ALU.subtract
            )

        def sigmoid_tile(a):
            nc.scalar.activation(out=share[:, a, :], in_=share[:, a, :], func=ACT.Sigmoid, scale=-2.0)

        def d_times_share_tile(a):
            nc.gpsimd.tensor_tensor(out=d_share[:, a, :], in0=d[:, a, :], in1=share[:, a, :], op=ALU.mult)

        def sigmoid(k):
            nc.scalar.activation(out=share[:, group(k), :], in_=share[:, group(k), :], func=ACT.Sigmoid, scale=-2.0)

        def d_over_e1(k):
            nc.vector.scalar_tensor_tensor(
                out=quad[:, group(k), :],
                in0=d[:, group(k), :],
                scalar=-1.0,
                in1=for_each_tile(turned[INV_E1]),
                op0=ALU.mult,
                op1=ALU.mult,
            )

        def d_times_share(k):
            nc.gpsimd.tensor_tensor(
                out=d_share[:, group(k), :], in0=d[:, group(k), :], in1=share[:, group(k), :], op=ALU.mult
            )

        def finish_quad(k):
            nc.gpsimd.tensor_tensor(
                out=quad[:, group(k), :], in0=quad[:, group(k), :], in1=d_share[:, group(k), :], op=ALU.mult
            )

        def new_banks():
            return [bank_ps.tile([P, BANK], F32, name="back", tag="bank") for r in range(ROW_TILES)]

        def turn_back(src, k, banks):
            for r in range(ROW_TILES):
                for a in range(k * PER_GROUP, (k + 1) * PER_GROUP):
                    slot = a % (COL_TILES // HALVES)
                    nc.tensor.transpose(banks[r][:, slot * P : (slot + 1) * P], src[:, a, rows(r)], ident[:])

        def by_label(ap, width):
            return ap.rearrange("p (i c) -> p i c", c=width)

        def for_each_label(table, r, width, n_labels):
            return table[:, r, :].unsqueeze(1).to_broadcast([P, n_labels, width])

        def finish_mu(h, banks, lo, hi, store):
            for r in range(ROW_TILES):
                nc.vector.scalar_tensor_tensor(
                    out=by_label(mu_sb[:, r, h * BANK + lo : h * BANK + hi], TABLE),
                    in0=by_label(banks[r][:, lo:hi], TABLE),
                    scalar=1.0,
                    in1=for_each_label(tabs[:, MEAN], r, TABLE, (hi - lo) // TABLE),
                    op0=ALU.subtract,
                    op1=ALU.add,
                )
                if store:
                    nc.sync.dma_start(out=mu_out[:, r, cols(h)], in_=mu_sb[:, r, cols(h)])

        def finish_var(h, banks):
            for r in range(ROW_TILES):
                nc.vector.scalar_tensor_tensor(
                    out=by_label(var_sb[:, r, cols(h)], TABLE),
                    in0=by_label(banks[r][:], TABLE),
                    scalar=0.5,
                    in1=for_each_label(v1_tab, r, TABLE, BANK // TABLE),
                    op0=ALU.mult,
                    op1=ALU.add,
                )
                nc.sync.dma_start(out=var_out[:, r, cols(h)], in_=var_sb[:, r, cols(h)])

        def turn_pairs(src, k, banks, first, last):
            for r in range(ROW_TILES):
                for a in range(k * PER_GROUP, (k + 1) * PER_GROUP):
                    slot = a % (COL_TILES // HALVES)
                    nc.tensor.matmul(
                        out=banks[r][:, slot * P : (slot + 1) * P],
                        lhsT=src[:, a, rows(r)],
                        rhs=perm[:],
                        start=(first and a % PER_GROUP == 0),
                        stop=(last and a % PER_GROUP == PER_GROUP - 1),
                        is_transpose=True,
                    )

        def finish_scale(h, banks):
            half = slice(h * BANK // GAUSS, (h + 1) * BANK // GAUSS)

            def by_g(r, g):
                return banks[r][:].rearrange("p (s g c) -> p s g c", g=GAUSS, c=PAIRS)[:, :, g, :]

            def first_step(r):
                nc.vector.scalar_tensor_tensor(
                    out=by_label(half_sum[:, r, half], PAIRS),
                    in0=by_g(r, 0),
                    scalar=0.5,
                    in1=for_each_label(c_twice, r, PAIRS, COL_TILES // HALVES),
                    op0=ALU.mult,
                    op1=ALU.add,
                )

            def second_step(r):
                nc.vector.scalar_tensor_tensor(
                    out=by_label(scale_sb[:, r, half], PAIRS),
                    in0=by_g(r, 1),
                    scalar=0.5,
                    in1=by_label(half_sum[:, r, half], PAIRS),
                    op0=ALU.mult,
                    op1=ALU.add,
                )
                nc.sync.dma_start(out=scale_out[:, r, half], in_=scale_sb[:, r, half])

            first_step(0)
            for r in range(1, ROW_TILES):
                first_step(r)
                second_step(r - 1)
            second_step(ROW_TILES - 1)

        def log_of_rest(k):
            nc.scalar.activation(
                out=log_rest[:, group(k), :], in_=share[:, group(k), :], func=ACT.Ln, bias=one_col[:], scale=-1.0
            )

        def log_of_share(k):
            nc.scalar.activation(out=log_share[:, group(k), :], in_=share[:, group(k), :], func=ACT.Ln)

        mu_banks = [None, None]
        turn_table(LOGSTD)
        bias_t = bank_ps.tile([P, P], BF16, name="bias_t", tag="bank")
        nc.tensor.transpose(bias_t[:], bias_rows[:], ident_bf[:])
        nc.scalar.activation(out=bias1[:], in_=bias_t[:, 0 : 2 * COL_TILES], func=ACT.Identity, bias=one_col[:])
        project(LOGSTD, 0)
        for a in range(PER_GROUP):
            minus_state_tile(LOGSTD, a)
        project(MEAN, 0)
        turn_table(MEAN)
        for a in range(PER_GROUP):
            minus_state_tile(MEAN, a)
        for a in range(PER_GROUP):
            sigmoid_tile(a)
        for a in range(PER_GROUP):
            d_times_share_tile(a)
        turn_table(INV_E1)
        d_over_e1(0)
        finish_quad(0)
        project(LOGSTD, 1)
        minus_state(LOGSTD, 1)
        for k in range(1, GROUPS):
            project(MEAN, k)
            if k == 3:
                mu_banks[0] = new_banks()
                turn_back(d_share, 0, mu_banks[0])
                turn_back(d_share, 1, mu_banks[0])
            minus_state(MEAN, k)
            if k + 1 < GROUPS:
                project(LOGSTD, k + 1)
                minus_state(LOGSTD, k + 1)
            if k == 3:
                finish_mu(0, mu_banks[0], 0, BANK, True)
            sigmoid(k)
            d_over_e1(k)
            d_times_share(k)
        for k in range(1, GROUPS):
            finish_quad(k)

        pair_banks = [new_banks(), None]
        for r in range(2):
            nc.tensor.matmul(out=pair_banks[0][r][:], lhsT=zeros[:, 0:P], rhs=zeros[:], start=True, stop=True)
        turn_pairs(quad, 0, pair_banks[0], True, False)
        mu_banks[1] = new_banks()
        turn_back(d_share, 2, mu_banks[1])
        turn_back(d_share, 3, mu_banks[1])
        finish_mu(1, mu_banks[1], 0, BANK, True)
        var_banks = new_banks()
        for k in (0, 1):
            log_of_rest(k)
            turn_back(log_rest, k, var_banks)
        finish_var(0, var_banks)
        log_of_share(0)
        turn_pairs(log_share, 0, pair_banks[0], False, False)
        turn_pairs(quad, 1, pair_banks[0], False, False)
        log_of_share(1)
        turn_pairs(log_share, 1, pair_banks[0], False, True)
        finish_scale(0, pair_banks[0])
        var_banks = new_banks()
        log_of_rest(2)
        turn_back(log_rest, 2, var_banks)
        pair_banks[1] = new_banks()
        turn_pairs(quad, 2, pair_banks[1], True, False)
        log_of_rest(3)
        turn_back(log_rest, 3, var_banks)
        finish_var(1, var_banks)
        log_of_share(2)
        turn_pairs(log_share, 2, pair_banks[1], False, False)
        log_of_share(3)
        turn_pairs(log_share, 3, pair_banks[1], False, False)
        turn_pairs(quad, 3, pair_banks[1], False, True)
        finish_scale(1, pair_banks[1])
